import numpy as np
import ml_dtypes


def mxq(x, axis, fmt="e4m3"):
    dtype, down = {"e4m3": (ml_dtypes.float8_e4m3fn, 7), "e5m2": (ml_dtypes.float8_e5m2, 14)}[fmt]
    v = np.moveaxis(np.asarray(x, np.float32).astype(ml_dtypes.bfloat16).astype(np.float64), axis, -1)
    blocks = v.reshape(v.shape[:-1] + (-1, 32))
    amax = np.abs(blocks).max(-1, keepdims=True)
    byte = np.maximum(np.where(amax > 0, np.frexp(amax)[1] - 1 + 127, 0) - down, 1)
    scale = np.exp2(byte - 127.0)
    codes = (blocks / scale).astype(np.float32).astype(dtype).astype(np.float64)
    return np.moveaxis((codes * scale).reshape(v.shape), -1, axis)


WIDE = False


def mx_kscale(k):
    if not WIDE:
        return np.ones(k)
    levels = np.array([10, -10, 5, -5, 0])
    a = np.random.permutation(np.resize(levels, k // 512 * 4)).reshape(k // 512, 4)
    idx = np.arange(k)
    return np.exp2(a[idx // 512, idx % 128 // 32])


BF16 = ml_dtypes.bfloat16


def bf(x):
    return np.asarray(x, np.float32).astype(BF16)


def f64(x):
    return np.asarray(x).astype(np.float64)


B, N, D, K = 16, 1024, 512, 64
EPS = 1e-12


def setup_inputs():
    s = mx_kscale(N)
    r = s / s.min()
    x = np.random.standard_normal((B, N, D)) * s[None, :, None]
    z = np.random.standard_normal((B * N, K)) * 2.0
    z[:, 0] = np.log(np.exp(z[:, 0]) + (np.tile(r, B) - 1.0) * np.exp(z).sum(-1))
    g = s.min() / np.mean(1.0 / r)
    c = np.random.standard_normal((1, D, K)) * 6.0 / np.sqrt(N) * g
    return {"x": bf(x), "bn_out": bf(z), "clusters2": bf(c)}


def reference(x, bn_out, clusters2):
    z = f64(bn_out)
    e = np.exp(z - z.max(-1, keepdims=True))
    P = (e / e.sum(-1, keepdims=True)).reshape(B, N, K)
    a_sum = P.sum(axis=1)
    vlad = mxq(P, 1, "e4m3").transpose(0, 2, 1) @ mxq(f64(x), 1, "e4m3")
    c2 = f64(clusters2)[0].T
    vlad = vlad - a_sum[:, :, None] * c2[None]
    vlad = vlad * (1.0 / np.sqrt((vlad * vlad).sum(-1, keepdims=True) + EPS))
    out = vlad.transpose(0, 2, 1).reshape(B, D * K)
    out = out * (1.0 / np.sqrt((out * out).sum(-1, keepdims=True) + EPS))
    return out

@@ -1,0 +1,339 @@
+from contextlib import ExitStack
+
+import concourse.mybir as mybir
+from concourse.masks import make_identity
+
+F32 = mybir.dt.float32
+BF16 = mybir.dt.bfloat16
+U32 = mybir.dt.uint32
+U8 = mybir.dt.uint8
+I32 = mybir.dt.int32
+FP8X4 = mybir.dt.float8_e4m3fn_x4
+ALU = mybir.AluOpType
+ACT = mybir.ActivationFunctionType
+AX = mybir.AxisListType
+
+B, N, D, K = 16, 1024, 512, 64
+EPS = 1e-12
+P = 128
+PACK = 4
+PASSES = N // (P * PACK)
+NPAIR = B // 2
+XBUFS = 8
+VD = [32] * B
+ZCHUNKS = [(0, 1), (1, 2), (2, 4), (4, 6), (6, 8)]
+
+FLOPS = 2 * B * N * K * D
+
+
+def tile_modelnew_kernel(tc, x, bn_out, clusters2, out):
+    nc = tc.nc
+    with ExitStack() as ctx:
+        const = ctx.enter_context(tc.tile_pool(name="const", bufs=1))
+        xpool = ctx.enter_context(tc.tile_pool(name="xraw", bufs=XBUFS))
+        gpool = ctx.enter_context(tc.tile_pool(name="grouped", bufs=4))
+        wpool = ctx.enter_context(tc.tile_pool(name="xwords", bufs=4))
+        spool = ctx.enter_context(tc.tile_pool(name="soft", bufs=3))
+        mpool = ctx.enter_context(tc.tile_pool(name="maxes", bufs=2))
+        epool = ctx.enter_context(tc.tile_pool(name="epi", bufs=3))
+        tiny = ctx.enter_context(tc.tile_pool(name="tiny", bufs=4))
+        ps_acc = ctx.enter_context(tc.psum_pool(name="ps_acc", bufs=2))
+        ps_tr = ctx.enter_context(tc.psum_pool(name="ps_tr", bufs=2))
+        ps_as = ctx.enter_context(tc.psum_pool(name="ps_as", bufs=2))
+        ps_tot = ctx.enter_context(tc.psum_pool(name="ps_tot", bufs=2))
+        ctx.enter_context(tc.manual_schedule())
+
+        zt = const.tile([P, B * PASSES, PACK, K], BF16)
+        negmax = const.tile([P, B * PASSES * PACK], F32)
+        pw = const.tile([P, NPAIR, PASSES, 192], U32, align_bytes=64)
+        pscale = const.tile([P, NPAIR, PASSES, 192], U8, align_bytes=64)
+        ident = const.tile([P, P], F32)
+        allones = const.tile([P, P], F32)
+        mask = const.tile([P, 2], F32)
+        neghalf = const.tile([P, 2], F32)
+        negone = const.tile([P, 1], F32)
+        c2raw = const.tile([P, PACK, K], BF16)
+        c2dup = const.tile([P, PACK, 2, K], F32)
+        negc2t = const.tile([P, PACK, P], F32)
+
+        zview = bn_out.rearrange("(s p j) k -> p s (j k)", p=P, j=PACK)
+
+        def load_z(ch):
+            s0 = ZCHUNKS[ch][0] * 2 * PASSES
+            s1 = ZCHUNKS[ch][1] * 2 * PASSES
+            nc.sync.dma_start(
+                out=zt[:, s0:s1, :, :].rearrange("p s j k -> p s (j k)"), in_=zview[:, s0:s1, :]
+            )
+
+        xraw = {}
+
+        def load_x(b):
+            raw = xpool.tile([P, PASSES, PACK, D], BF16, name="raw")
+            nc.sync.dma_start(
+                out=raw[:].rearrange("p c j d -> p c (j d)"),
+                in_=x[b].rearrange("(c p j) d -> p c (j d)", c=PASSES, p=P, j=PACK),
+            )
+            xraw[b] = raw
+
+        def maxes(ch):
+            s0 = ZCHUNKS[ch][0] * 2 * PASSES
+            s1 = ZCHUNKS[ch][1] * 2 * PASSES
+            ns = (s1 - s0) * PACK
+            zc = zt[:, s0:s1, :, :].rearrange("p s j k -> p (s j) k")
+            t1 = mpool.tile([P, ns, 32], BF16, name="t1")
+            nc.vector.tensor_tensor(out=t1[:], in0=zc[:, :, 0:32], in1=zc[:, :, 32:64], op=ALU.max)
+            t2 = mpool.tile([P, ns, 16], BF16, name="t2")
+            nc.vector.tensor_tensor(out=t2[:], in0=t1[:, :, 0:16], in1=t1[:, :, 16:32], op=ALU.max)
+            t3 = mpool.tile([P, ns, 8], BF16, name="t3")
+            nc.vector.tensor_tensor(out=t3[:], in0=t2[:, :, 0:8], in1=t2[:, :, 8:16], op=ALU.max)
+            nc.vector.tensor_reduce(
+                out=negmax[:, s0 * PACK : s1 * PACK], in_=t3[:], axis=AX.X, op=ALU.max, negate=True
+            )
+
+        soft = {}
+
+        def exps(pr, b2):
+            if b2 == 0:
+                e = spool.tile([P, PASSES, PACK, 2, K], F32, name="e")
+                sums = tiny.tile([P, PASSES, PACK, 2], F32, name="sums")
+                soft[pr] = (e, sums)
+            e, sums = soft[pr]
+            for c in range(PASSES):
+                s = (2 * pr + b2) * PASSES + c
+                for j in range(PACK):
+                    i = s * PACK + j
+                    nc.scalar.activation(
+                        out=e[:, c, j, b2, :],
+                        in_=zt[:, s, j, :],
+                        func=ACT.Exp,
+                        bias=negmax[:, i : i + 1],
+                        scale=1.0,
+                        accum_out=sums[:, c, j, b2 : b2 + 1],
+                    )
+
+        pgs = {}
+        asum = {}
+
+        def soft_a(pr):
+            e, sums = soft[pr]
+            rinv = tiny.tile([P, PASSES, PACK, 2], F32, name="rinv")
+            nc.vector.reciprocal(out=rinv[:], in_=sums[:])
+            asps = ps_as.tile([P, 2], F32, name="asps")
+            for c in range(PASSES):
+                for j in range(PACK):
+                    nc.tensor.matmul(
+                        out=asps[:],
+                        lhsT=e[:, c, j, :, :].rearrange("p b k -> p (b k)"),
+                        rhs=rinv[:, c, j, :],
+                        start=(c == 0 and j == 0),
+                        stop=(c == PASSES - 1 and j == PACK - 1),
+                    )
+            pg = spool.tile([P, 2, PASSES, K, PACK], BF16, name="pg", align_bytes=64)
+            for b2 in range(2):
+                nc.vector.tensor_tensor(
+                    out=pg[:, b2],
+                    in0=e[:, :, :, b2, :].rearrange("p c j k -> p c k j"),
+                    in1=rinv[:, :, :, b2].unsqueeze(2).to_broadcast([P, PASSES, K, PACK]),
+                    op=ALU.mult,
+                )
+            pgs[pr] = (pg, asps)
+
+        def soft_b(pr):
+            pg, asps = pgs[pr]
+            for b2 in range(2):
+                for c in range(PASSES):
+                    nc.vector.quantize_mx(
+                        out=pw[:, pr, c, 128 * b2 : 128 * b2 + K].bitcast(FP8X4),
+                        scales=pscale[:, pr, c, 128 * b2 : 128 * b2 + K],
+                        in_=pg[:, b2, c, :, :].rearrange("p k j -> p (k j)"),
+                    )
+
+        def acopy(pr):
+            asps = pgs[pr][1]
+            a = tiny.tile([P, 1], F32, name="a")
+            nc.vector.tensor_copy(out=a[0:64, :], in_=asps[0:64, 0:1])
+            nc.vector.tensor_copy(out=a[64:128, :], in_=asps[64:128, 1:2])
+            asum[pr] = a
+
+        groupeds = {}
+
+        def regroup(copy, b, c, d0, d1):
+            copy(
+                out=groupeds[b][:, c, d0:d1, :].rearrange("p (w i) t -> p w t i", i=4),
+                in_=xraw[b][:, c, :, d0:d1].rearrange("p t (w i) -> p w t i", i=4),
+            )
+
+        def regroup_v(b):
+            groupeds[b] = gpool.tile([P, PASSES, D, PACK], BF16, name="grouped", align_bytes=64)
+            regroup(nc.vector.tensor_copy, b, 0, 0, D)
+            if VD[b] > 0:
+                regroup(nc.vector.tensor_copy, b, 1, 0, VD[b])
+
+        def regroup_s(b):
+            regroup(nc.scalar.copy, b, 1, VD[b], D)
+
+        st = {}
+
+        def quant_x(b):
+            pr = b // 2
+            b2 = b % 2
+            xw = wpool.tile([P, PASSES, D], U32, name="xw", align_bytes=64)
+            xs = wpool.tile([P, PASSES, D], U8, name="xs", align_bytes=64)
+            if b2 == 0:
+                st[pr] = {"acc": ps_acc.tile([P, D], F32, name="acc")}
+            for c in range(PASSES):
+                nc.vector.quantize_mx(
+                    out=xw[:, c, :].bitcast(FP8X4),
+                    scales=xs[:, c, :],
+                    in_=groupeds[b][:, c, :, :].rearrange("p d t -> p (d t)"),
+                )
+            for c in range(PASSES):
+                nc.tensor.matmul_mx(
+                    out=st[pr]["acc"][:],
+                    lhsT=pw[:, pr, c, 64 * b2 : 64 * b2 + P].bitcast(FP8X4),
+                    lhsT_scale=pscale[:, pr, c, 64 * b2 : 64 * b2 + P],
+                    rhs=xw[:, c, :].bitcast(FP8X4),
+                    rhs_scale=xs[:, c, :],
+                    start=(b2 == 0 and c == 0),
+                    stop=(b2 == 1 and c == PASSES - 1),
+                )
+
+        def stt(pr):
+            v = epool.tile([P, PACK, P], F32, name="v")
+            nc.vector.scalar_tensor_tensor(
+                out=v[:],
+                in0=negc2t[:],
+                scalar=asum[pr][:, 0:1],
+                in1=st[pr]["acc"][:].rearrange("p (q c) -> p c q", c=PACK),
+                op0=ALU.mult,
+                op1=ALU.add,
+            )
+            st[pr]["v"] = v
+
+        def square(pr):
+            junk = epool.tile([P, PACK, P], BF16, name="junk")
+            ssq = tiny.tile([P, 1], F32, name="ssq")
+            nc.scalar.activation(out=junk[:], in_=st[pr]["v"][:], func=ACT.Square, accum_out=ssq[:])
+            t = tiny.tile([P, 1], F32, name="t")
+            nc.gpsimd.tensor_scalar(out=t[:], in0=ssq[:], scalar1=EPS, scalar2=1.0, op0=ALU.add, op1=ALU.mult)
+            rn = tiny.tile([P, 1], F32, name="rn")
+            nc.gpsimd.tensor_tensor(out=rn[:], in0=t[:], in1=neghalf[:, 0:1], op=ALU.pow)
+            rt = tiny.tile([P, 1], F32, name="rt")
+            nc.gpsimd.tensor_tensor(out=rt[:], in0=t[:], in1=negone[:], op=ALU.pow)
+            q2 = tiny.tile([P, 2], F32, name="q2")
+            nc.gpsimd.tensor_scalar(
+                out=q2[:], in0=mask[:], scalar1=ssq[:, 0:1], scalar2=rt[:, 0:1], op0=ALU.mult, op1=ALU.mult
+            )
+            totps = ps_tot.tile([P, 2], F32, name="totps")
+            nc.tensor.matmul(out=totps[:], lhsT=allones[:], rhs=q2[:], start=True, stop=True)
+            st[pr]["rn"] = rn
+            st[pr]["totps"] = totps
+
+        def total(pr):
+            tt = tiny.tile([P, 2], F32, name="tt")
+            nc.vector.tensor_scalar(out=tt[:], in0=st[pr]["totps"][:], scalar1=EPS, scalar2=None, op0=ALU.add)
+            r2 = tiny.tile([P, 2], F32, name="r2")
+            nc.gpsimd.tensor_tensor(out=r2[:], in0=tt[:], in1=neghalf[:], op=ALU.pow)
+            st[pr]["r2"] = r2
+
+        def scale(pr):
+            vs = epool.tile([P, PACK, P], F32, name="vs")
+            nc.scalar.activation(out=vs[:], in_=st[pr]["v"][:], func=ACT.Copy, scale=st[pr]["rn"][:, 0:1])
+            trps = ps_tr.tile([P, PACK, P], F32, name="trps")
+            for ch in range(PACK):
+                nc.tensor.transpose(trps[:, ch, :], vs[:, ch, :], ident[:])
+            st[pr]["trps"] = trps
+
+        def finish(pr):
+            o = epool.tile([P, 2, PACK, K], F32, name="o")
+            for b2 in range(2):
+                nc.scalar.activation(
+                    out=o[:, b2],
+                    in_=st[pr]["trps"][:, :, K * b2 : K * b2 + K],
+                    func=ACT.Copy,
+                    scale=st[pr]["r2"][:, b2 : b2 + 1],
+                )
+            nc.scalar.dma_start(
+                out=out[2 * pr : 2 * pr + 2, :].rearrange("b (q r) -> q b r", q=P),
+                in_=o[:].rearrange("p b c k -> p b (c k)"),
+            )
+
+        load_z(0)
+        nc.sync.dma_start(
+            out=c2raw[:].rearrange("p c k -> p (c k)"),
+            in_=clusters2[0].rearrange("(q c) k -> q (c k)", c=PACK),
+        )
+        load_x(0)
+        load_z(1)
+        load_x(1)
+        load_z(2)
+        load_x(2)
+        load_x(3)
+        load_z(3)
+        load_x(4)
+        load_x(5)
+        load_z(4)
+        load_x(6)
+        load_x(7)
+
+        nc.vector.memset(pw[:, :, :, 64:128].bitcast(I32), 0)
+        nc.vector.memset(pscale[:, :, :, 64:128].bitcast(I32), 0)
+        make_identity(nc, ident[:])
+        nc.gpsimd.memset(allones[:], 1.0)
+        nc.gpsimd.memset(mask[:], 0.0)
+        nc.gpsimd.memset(mask[0:64, 0:1], 1.0)
+        nc.gpsimd.memset(mask[64:128, 1:2], 1.0)
+        nc.gpsimd.memset(neghalf[:], -0.5)
+        nc.gpsimd.memset(negone[:], -1.0)
+
+        chunk_at = {-3: 0, 0: 1}
+        for ch in range(2, len(ZCHUNKS)):
+            chunk_at[2 * ZCHUNKS[ch][0] - 3] = ch
+
+        def pair_of(t, lag):
+            if (t - lag) % 2 != 0:
+                return None
+            pr = (t - lag) // 2
+            return pr if 0 <= pr < NPAIR else None
+
+        def at(t, lag, step):
+            pr = pair_of(t, lag)
+            if pr is not None:
+                step(pr)
+
+        for t in range(-3, B + 7):
+            if 0 <= t < B:
+                regroup_v(t)
+                regroup_s(t)
+                if t + XBUFS < B:
+                    load_x(t + XBUFS)
+            if t in chunk_at:
+                maxes(chunk_at[t])
+            if t == -3:
+                nc.vector.tensor_scalar(
+                    out=c2dup[:],
+                    in0=c2raw[:].unsqueeze(2).to_broadcast([P, PACK, 2, K]),
+                    scalar1=-1.0,
+                    scalar2=None,
+                    op0=ALU.mult,
+                )
+                c2ps = ps_tr.tile([P, PACK, P], F32, name="trps")
+                for ch in range(PACK):
+                    nc.tensor.transpose(
+                        c2ps[:, ch, :], c2dup[:, ch, :, :].rearrange("p b k -> p (b k)"), ident[:]
+                    )
+            at(t, 1, soft_b)
+            if 0 <= t - 1 < B:
+                quant_x(t - 1)
+            if t == 1:
+                nc.vector.tensor_copy(out=negc2t[:], in_=c2ps[:])
+            at(t, 2, acopy)
+            pe = (t + 2) // 2
+            if 0 <= pe < NPAIR:
+                exps(pe, (t + 2) % 2)
+            at(t, 3, stt)
+            at(t, 4, square)
+            at(t, 5, total)
+            at(t, 0, soft_a)
+            at(t, 5, scale)
+            at(t, 6, finish)

@@ -20,7 +20,7 @@ PACK = 4
 PASSES = N // (P * PACK)
 NPAIR = B // 2
 XBUFS = 8
-VD = [32] * B
+VD = [288] * B
 ZCHUNKS = [(0, 1), (1, 2), (2, 4), (4, 6), (6, 8)]
 
 FLOPS = 2 * B * N * K * D

@@ -20,7 +20,7 @@ PACK = 4
 PASSES = N // (P * PACK)
 NPAIR = B // 2
 XBUFS = 8
-VD = [288] * B
+NV = [224, 288] + [576] * 13 + [512]
 ZCHUNKS = [(0, 1), (1, 2), (2, 4), (4, 6), (6, 8)]
 
 FLOPS = 2 * B * N * K * D
@@ -37,21 +37,39 @@ def tile_modelnew_kernel(tc, x, bn_out, clusters2, out):
         mpool = ctx.enter_context(tc.tile_pool(name="maxes", bufs=2))
         epool = ctx.enter_context(tc.tile_pool(name="epi", bufs=3))
         tiny = ctx.enter_context(tc.tile_pool(name="tiny", bufs=4))
+        keep = ctx.enter_context(tc.tile_pool(name="keep", bufs=NPAIR))
         ps_acc = ctx.enter_context(tc.psum_pool(name="ps_acc", bufs=2))
         ps_tr = ctx.enter_context(tc.psum_pool(name="ps_tr", bufs=2))
-        ps_as = ctx.enter_context(tc.psum_pool(name="ps_as", bufs=2))
+        ps_as = ctx.enter_context(tc.psum_pool(name="ps_as", bufs=1))
         ps_tot = ctx.enter_context(tc.psum_pool(name="ps_tot", bufs=2))
         ctx.enter_context(tc.manual_schedule())
 
-        zt = const.tile([P, B * PASSES, PACK, K], BF16)
-        negmax = const.tile([P, B * PASSES * PACK], F32)
-        pw = const.tile([P, NPAIR, PASSES, 192], U32, align_bytes=64)
-        pscale = const.tile([P, NPAIR, PASSES, 192], U8, align_bytes=64)
+        zts = []
+        negmaxes = []
+        for ch in range(len(ZCHUNKS)):
+            ns = (ZCHUNKS[ch][1] - ZCHUNKS[ch][0]) * 2 * PASSES
+            zts.append(const.tile([P, ns, PACK, K], BF16, name="zt%d" % ch))
+            negmaxes.append(const.tile([P, ns * PACK], F32, name="negmax%d" % ch))
+        chunk_of = {}
+        for ch in range(len(ZCHUNKS)):
+            for pr in range(ZCHUNKS[ch][0], ZCHUNKS[ch][1]):
+                chunk_of[pr] = ch
+        es = []
+        sumss = []
+        rinvs = []
+        pws = []
+        pscales = []
+        for pr in range(NPAIR):
+            es.append(keep.tile([P, PASSES, PACK, 2, K], F32, name="e"))
+            sumss.append(keep.tile([P, PASSES, PACK, 2], F32, name="sums"))
+            rinvs.append(keep.tile([P, PASSES, PACK, 2], F32, name="rinv"))
+            pws.append(keep.tile([P, PASSES, 192], U32, name="pw", align_bytes=64))
+            pscales.append(keep.tile([P, PASSES, 192], U8, name="pscale", align_bytes=64))
+        asum = const.tile([P, NPAIR], F32)
+        asps = [ps_as.tile([P, 4, 2], F32, name="asps0"), ps_as.tile([P, 4, 2], F32, name="asps1")]
         ident = const.tile([P, P], F32)
-        allones = const.tile([P, P], F32)
         mask = const.tile([P, 2], F32)
-        neghalf = const.tile([P, 2], F32)
-        negone = const.tile([P, 1], F32)
+        eps_t = const.tile([P, 1], F32)
         c2raw = const.tile([P, PACK, K], BF16)
         c2dup = const.tile([P, PACK, 2, K], F32)
         negc2t = const.tile([P, PACK, P], F32)
@@ -61,116 +79,108 @@ def tile_modelnew_kernel(tc, x, bn_out, clusters2, out):
         def load_z(ch):
             s0 = ZCHUNKS[ch][0] * 2 * PASSES
             s1 = ZCHUNKS[ch][1] * 2 * PASSES
-            nc.sync.dma_start(
-                out=zt[:, s0:s1, :, :].rearrange("p s j k -> p s (j k)"), in_=zview[:, s0:s1, :]
-            )
+            nc.sync.dma_start(out=zts[ch][:].rearrange("p s j k -> p s (j k)"), in_=zview[:, s0:s1, :])
 
         xraw = {}
 
         def load_x(b):
             raw = xpool.tile([P, PASSES, PACK, D], BF16, name="raw")
-            nc.sync.dma_start(
-                out=raw[:].rearrange("p c j d -> p c (j d)"),
-                in_=x[b].rearrange("(c p j) d -> p c (j d)", c=PASSES, p=P, j=PACK),
-            )
+            xv = x[b].rearrange("(c p j) d -> c p (j d)", c=PASSES, p=P, j=PACK)
+            for c in range(PASSES):
+                nc.sync.dma_start(out=raw[:, c, :, :].rearrange("p j d -> p (j d)"), in_=xv[c])
             xraw[b] = raw
 
-        def maxes(ch):
-            s0 = ZCHUNKS[ch][0] * 2 * PASSES
-            s1 = ZCHUNKS[ch][1] * 2 * PASSES
-            ns = (s1 - s0) * PACK
-            zc = zt[:, s0:s1, :, :].rearrange("p s j k -> p (s j) k")
+        def max_steps(ch):
+            ns = (ZCHUNKS[ch][1] - ZCHUNKS[ch][0]) * 2 * PASSES * PACK
+            zc = zts[ch][:].rearrange("p s j k -> p (s j) k")
             t1 = mpool.tile([P, ns, 32], BF16, name="t1")
-            nc.vector.tensor_tensor(out=t1[:], in0=zc[:, :, 0:32], in1=zc[:, :, 32:64], op=ALU.max)
             t2 = mpool.tile([P, ns, 16], BF16, name="t2")
-            nc.vector.tensor_tensor(out=t2[:], in0=t1[:, :, 0:16], in1=t1[:, :, 16:32], op=ALU.max)
             t3 = mpool.tile([P, ns, 8], BF16, name="t3")
-            nc.vector.tensor_tensor(out=t3[:], in0=t2[:, :, 0:8], in1=t2[:, :, 8:16], op=ALU.max)
-            nc.vector.tensor_reduce(
-                out=negmax[:, s0 * PACK : s1 * PACK], in_=t3[:], axis=AX.X, op=ALU.max, negate=True
-            )
+            return [
+                lambda: nc.vector.tensor_tensor(out=t1[:], in0=zc[:, :, 0:32], in1=zc[:, :, 32:64], op=ALU.max),
+                lambda: nc.vector.tensor_tensor(out=t2[:], in0=t1[:, :, 0:16], in1=t1[:, :, 16:32], op=ALU.max),
+                lambda: nc.vector.tensor_tensor(out=t3[:], in0=t2[:, :, 0:8], in1=t2[:, :, 8:16], op=ALU.max),
+                lambda: nc.vector.tensor_reduce(
+                    out=negmaxes[ch][:], in_=t3[:], axis=AX.X, op=ALU.max, negate=True
+                ),
+            ]
 
-        soft = {}
-
-        def exps(pr, b2):
-            if b2 == 0:
-                e = spool.tile([P, PASSES, PACK, 2, K], F32, name="e")
-                sums = tiny.tile([P, PASSES, PACK, 2], F32, name="sums")
-                soft[pr] = (e, sums)
-            e, sums = soft[pr]
-            for c in range(PASSES):
-                s = (2 * pr + b2) * PASSES + c
-                for j in range(PACK):
-                    i = s * PACK + j
-                    nc.scalar.activation(
-                        out=e[:, c, j, b2, :],
-                        in_=zt[:, s, j, :],
-                        func=ACT.Exp,
-                        bias=negmax[:, i : i + 1],
-                        scale=1.0,
-                        accum_out=sums[:, c, j, b2 : b2 + 1],
-                    )
+        def exps(pr):
+            ch = chunk_of[pr]
+            for b2 in range(2):
+                for c in range(PASSES):
+                    s = (2 * (pr - ZCHUNKS[ch][0]) + b2) * PASSES + c
+                    for j in range(PACK):
+                        i = s * PACK + j
+                        nc.scalar.activation(
+                            out=es[pr][:, c, j, b2, :],
+                            in_=zts[ch][:, s, j, :],
+                            func=ACT.Exp,
+                            bias=negmaxes[ch][:, i : i + 1],
+                            scale=1.0,
+                            accum_out=sumss[pr][:, c, j, b2 : b2 + 1],
+                        )
 
         pgs = {}
-        asum = {}
 
-        def soft_a(pr):
-            e, sums = soft[pr]
-            rinv = tiny.tile([P, PASSES, PACK, 2], F32, name="rinv")
-            nc.vector.reciprocal(out=rinv[:], in_=sums[:])
-            asps = ps_as.tile([P, 2], F32, name="asps")
+        def recip(pr):
+            nc.vector.reciprocal(out=rinvs[pr][:], in_=sumss[pr][:])
+            pgs[pr] = spool.tile([P, 2, PASSES, K, PACK], BF16, name="pg", align_bytes=64)
+
+        def a_sum(pr):
             for c in range(PASSES):
                 for j in range(PACK):
                     nc.tensor.matmul(
-                        out=asps[:],
-                        lhsT=e[:, c, j, :, :].rearrange("p b k -> p (b k)"),
-                        rhs=rinv[:, c, j, :],
+                        out=asps[pr // 4][:, pr % 4, :],
+                        lhsT=es[pr][:, c, j, :, :].rearrange("p b k -> p (b k)"),
+                        rhs=rinvs[pr][:, c, j, :],
                         start=(c == 0 and j == 0),
                         stop=(c == PASSES - 1 and j == PACK - 1),
                     )
-            pg = spool.tile([P, 2, PASSES, K, PACK], BF16, name="pg", align_bytes=64)
+
+        def acopy(half):
             for b2 in range(2):
-                nc.vector.tensor_tensor(
-                    out=pg[:, b2],
-                    in0=e[:, :, :, b2, :].rearrange("p c j k -> p c k j"),
-                    in1=rinv[:, :, :, b2].unsqueeze(2).to_broadcast([P, PASSES, K, PACK]),
-                    op=ALU.mult,
+                nc.vector.tensor_copy(
+                    out=asum[64 * b2 : 64 * b2 + 64, 4 * half : 4 * half + 4],
+                    in_=asps[half][64 * b2 : 64 * b2 + 64, :, b2],
                 )
-            pgs[pr] = (pg, asps)
 
-        def soft_b(pr):
-            pg, asps = pgs[pr]
-            for b2 in range(2):
-                for c in range(PASSES):
-                    nc.vector.quantize_mx(
-                        out=pw[:, pr, c, 128 * b2 : 128 * b2 + K].bitcast(FP8X4),
-                        scales=pscale[:, pr, c, 128 * b2 : 128 * b2 + K],
-                        in_=pg[:, b2, c, :, :].rearrange("p k j -> p (k j)"),
-                    )
+        def norm(pr, b2):
+            nc.vector.tensor_tensor(
+                out=pgs[pr][:, b2],
+                in0=es[pr][:, :, :, b2, :].rearrange("p c j k -> p c k j"),
+                in1=rinvs[pr][:, :, :, b2].unsqueeze(2).to_broadcast([P, PASSES, K, PACK]),
+                op=ALU.mult,
+            )
 
-        def acopy(pr):
-            asps = pgs[pr][1]
-            a = tiny.tile([P, 1], F32, name="a")
-            nc.vector.tensor_copy(out=a[0:64, :], in_=asps[0:64, 0:1])
-            nc.vector.tensor_copy(out=a[64:128, :], in_=asps[64:128, 1:2])
-            asum[pr] = a
+        def quant_p(pr, i):
+            if pr < 0:
+                return
+            b2 = i // PASSES
+            c = i % PASSES
+            nc.vector.quantize_mx(
+                out=pws[pr][:, c, 128 * b2 : 128 * b2 + K].bitcast(FP8X4),
+                scales=pscales[pr][:, c, 128 * b2 : 128 * b2 + K],
+                in_=pgs[pr][:, b2, c, :, :].rearrange("p k j -> p (k j)"),
+            )
 
         groupeds = {}
 
         def regroup(copy, b, c, d0, d1):
-            copy(
-                out=groupeds[b][:, c, d0:d1, :].rearrange("p (w i) t -> p w t i", i=4),
-                in_=xraw[b][:, c, :, d0:d1].rearrange("p t (w i) -> p w t i", i=4),
-            )
+            if d0 < d1:
+                copy(
+                    out=groupeds[b][:, c, d0:d1, :].rearrange("p (w i) t -> p w t i", i=4),
+                    in_=xraw[b][:, c, :, d0:d1].rearrange("p t (w i) -> p w t i", i=4),
+                )
 
         def regroup_v(b):
             groupeds[b] = gpool.tile([P, PASSES, D, PACK], BF16, name="grouped", align_bytes=64)
-            regroup(nc.vector.tensor_copy, b, 0, 0, D)
-            if VD[b] > 0:
-                regroup(nc.vector.tensor_copy, b, 1, 0, VD[b])
+            regroup(nc.vector.tensor_copy, b, 0, 0, min(NV[b], D))
+            regroup(nc.vector.tensor_copy, b, 1, 0, NV[b] - D)
 
         def regroup_s(b):
-            regroup(nc.scalar.copy, b, 1, VD[b], D)
+            regroup(nc.scalar.copy, b, 0, NV[b], D)
+            regroup(nc.scalar.copy, b, 1, max(NV[b] - D, 0), D)
 
         st = {}
 
@@ -190,8 +200,8 @@ def tile_modelnew_kernel(tc, x, bn_out, clusters2, out):
             for c in range(PASSES):
                 nc.tensor.matmul_mx(
                     out=st[pr]["acc"][:],
-                    lhsT=pw[:, pr, c, 64 * b2 : 64 * b2 + P].bitcast(FP8X4),
-                    lhsT_scale=pscale[:, pr, c, 64 * b2 : 64 * b2 + P],
+                    lhsT=pws[pr][:, c, 64 * b2 : 64 * b2 + P].bitcast(FP8X4),
+                    lhsT_scale=pscales[pr][:, c, 64 * b2 : 64 * b2 + P],
                     rhs=xw[:, c, :].bitcast(FP8X4),
                     rhs_scale=xs[:, c, :],
                     start=(b2 == 0 and c == 0),
@@ -203,7 +213,7 @@ def tile_modelnew_kernel(tc, x, bn_out, clusters2, out):
             nc.vector.scalar_tensor_tensor(
                 out=v[:],
                 in0=negc2t[:],
-                scalar=asum[pr][:, 0:1],
+                scalar=asum[:, pr : pr + 1],
                 in1=st[pr]["acc"][:].rearrange("p (q c) -> p c q", c=PACK),
                 op0=ALU.mult,
                 op1=ALU.add,
@@ -214,27 +224,30 @@ def tile_modelnew_kernel(tc, x, bn_out, clusters2, out):
             junk = epool.tile([P, PACK, P], BF16, name="junk")
             ssq = tiny.tile([P, 1], F32, name="ssq")
             nc.scalar.activation(out=junk[:], in_=st[pr]["v"][:], func=ACT.Square, accum_out=ssq[:])
-            t = tiny.tile([P, 1], F32, name="t")
-            nc.gpsimd.tensor_scalar(out=t[:], in0=ssq[:], scalar1=EPS, scalar2=1.0, op0=ALU.add, op1=ALU.mult)
+            st[pr]["ssq"] = ssq
+
+        def rnorm(pr):
             rn = tiny.tile([P, 1], F32, name="rn")
-            nc.gpsimd.tensor_tensor(out=rn[:], in0=t[:], in1=neghalf[:, 0:1], op=ALU.pow)
-            rt = tiny.tile([P, 1], F32, name="rt")
-            nc.gpsimd.tensor_tensor(out=rt[:], in0=t[:], in1=negone[:], op=ALU.pow)
-            q2 = tiny.tile([P, 2], F32, name="q2")
-            nc.gpsimd.tensor_scalar(
-                out=q2[:], in0=mask[:], scalar1=ssq[:, 0:1], scalar2=rt[:, 0:1], op0=ALU.mult, op1=ALU.mult
+            nc.scalar.activation(
+                out=rn[:], in_=st[pr]["ssq"][:], func=ACT.Abs_reciprocal_sqrt, bias=eps_t[:, 0:1]
             )
-            totps = ps_tot.tile([P, 2], F32, name="totps")
-            nc.tensor.matmul(out=totps[:], lhsT=allones[:], rhs=q2[:], start=True, stop=True)
             st[pr]["rn"] = rn
-            st[pr]["totps"] = totps
 
         def total(pr):
-            tt = tiny.tile([P, 2], F32, name="tt")
-            nc.vector.tensor_scalar(out=tt[:], in0=st[pr]["totps"][:], scalar1=EPS, scalar2=None, op0=ALU.add)
-            r2 = tiny.tile([P, 2], F32, name="r2")
-            nc.gpsimd.tensor_tensor(out=r2[:], in0=tt[:], in1=neghalf[:], op=ALU.pow)
-            st[pr]["r2"] = r2
+            u = tiny.tile([P, 2], F32, name="u")
+            nc.vector.tensor_scalar(
+                out=u[:],
+                in0=mask[:],
+                scalar1=st[pr]["ssq"][:, 0:1],
+                scalar2=st[pr]["rn"][:, 0:1],
+                op0=ALU.mult,
+                op1=ALU.mult,
+            )
+            totps = ps_tot.tile([P, 2], F32, name="totps")
+            nc.tensor.matmul(
+                out=totps[:], lhsT=st[pr]["rn"][:, 0:1].to_broadcast([P, P]), rhs=u[:], start=True, stop=True
+            )
+            st[pr]["totps"] = totps
 
         def scale(pr):
             vs = epool.tile([P, PACK, P], F32, name="vs")
@@ -244,14 +257,22 @@ def tile_modelnew_kernel(tc, x, bn_out, clusters2, out):
                 nc.tensor.transpose(trps[:, ch, :], vs[:, ch, :], ident[:])
             st[pr]["trps"] = trps
 
+        def rtotal(pr):
+            r2 = tiny.tile([P, 2], F32, name="r2")
+            nc.scalar.activation(
+                out=r2[:], in_=st[pr]["totps"][:], func=ACT.Abs_reciprocal_sqrt, bias=eps_t[:, 0:1]
+            )
+            st[pr]["r2"] = r2
+
         def finish(pr):
+            r2 = st[pr]["r2"]
             o = epool.tile([P, 2, PACK, K], F32, name="o")
             for b2 in range(2):
                 nc.scalar.activation(
                     out=o[:, b2],
                     in_=st[pr]["trps"][:, :, K * b2 : K * b2 + K],
                     func=ACT.Copy,
-                    scale=st[pr]["r2"][:, b2 : b2 + 1],
+                    scale=r2[:, b2 : b2 + 1],
                 )
             nc.scalar.dma_start(
                 out=out[2 * pr : 2 * pr + 2, :].rearrange("b (q r) -> q b r", q=P),
@@ -259,81 +280,96 @@ def tile_modelnew_kernel(tc, x, bn_out, clusters2, out):
             )
 
         load_z(0)
+        load_z(1)
         nc.sync.dma_start(
             out=c2raw[:].rearrange("p c k -> p (c k)"),
             in_=clusters2[0].rearrange("(q c) k -> q (c k)", c=PACK),
         )
-        load_x(0)
-        load_z(1)
-        load_x(1)
         load_z(2)
-        load_x(2)
-        load_x(3)
         load_z(3)
-        load_x(4)
-        load_x(5)
         load_z(4)
-        load_x(6)
-        load_x(7)
+        for b in range(XBUFS):
+            load_x(b)
 
-        nc.vector.memset(pw[:, :, :, 64:128].bitcast(I32), 0)
-        nc.vector.memset(pscale[:, :, :, 64:128].bitcast(I32), 0)
+        for pr in range(NPAIR):
+            nc.vector.memset(pws[pr][:, :, 64:128].bitcast(I32), 0)
+            nc.vector.memset(pscales[pr][:, :, 64:128].bitcast(I32), 0)
         make_identity(nc, ident[:])
-        nc.gpsimd.memset(allones[:], 1.0)
         nc.gpsimd.memset(mask[:], 0.0)
         nc.gpsimd.memset(mask[0:64, 0:1], 1.0)
         nc.gpsimd.memset(mask[64:128, 1:2], 1.0)
-        nc.gpsimd.memset(neghalf[:], -0.5)
-        nc.gpsimd.memset(negone[:], -1.0)
+        nc.gpsimd.memset(eps_t[:], EPS)
 
-        chunk_at = {-3: 0, 0: 1}
-        for ch in range(2, len(ZCHUNKS)):
-            chunk_at[2 * ZCHUNKS[ch][0] - 3] = ch
+        for step in max_steps(0):
+            step()
+        exps(0)
+        m1 = max_steps(1)
+        m1[0]()
+        nc.vector.tensor_scalar(
+            out=c2dup[:],
+            in0=c2raw[:].unsqueeze(2).to_broadcast([P, PACK, 2, K]),
+            scalar1=-1.0,
+            scalar2=None,
+            op0=ALU.mult,
+        )
+        c2ps = ps_tr.tile([P, PACK, P], F32, name="trps")
+        for ch in range(PACK):
+            nc.tensor.transpose(c2ps[:, ch, :], c2dup[:, ch, :, :].rearrange("p b k -> p (b k)"), ident[:])
+        m1[1]()
+        m1[2]()
+        m1[3]()
+        exps(1)
+        for step in max_steps(2):
+            step()
+        later = max_steps(3) + max_steps(4)
 
-        def pair_of(t, lag):
-            if (t - lag) % 2 != 0:
-                return None
-            pr = (t - lag) // 2
-            return pr if 0 <= pr < NPAIR else None
+        def one_max(i):
+            if i < len(later):
+                later[i]()
+
+        for pr in range(NPAIR):
+            recip(pr)
+            if pr < 4:
+                a_sum(pr)
+            quant_p(pr - 1, 0)
+            one_max(4 * pr)
+            norm(pr, 0)
+            quant_p(pr - 1, 1)
+            one_max(4 * pr + 1)
+            norm(pr, 1)
+            quant_p(pr - 1, 2)
+            one_max(4 * pr + 2)
+            quant_p(pr - 1, 3)
+            one_max(4 * pr + 3)
+            if pr == 0:
+                nc.vector.tensor_copy(out=negc2t[:], in_=c2ps[:])
+            if pr + 2 < NPAIR:
+                exps(pr + 2)
+        for i in range(4):
+            quant_p(NPAIR - 1, i)
 
         def at(t, lag, step):
-            pr = pair_of(t, lag)
-            if pr is not None:
-                step(pr)
+            if (t - lag) % 2 == 0 and 0 <= (t - lag) // 2 < NPAIR:
+                step((t - lag) // 2)
 
-        for t in range(-3, B + 7):
-            if 0 <= t < B:
+        for t in range(B + 7):
+            if t < B:
                 regroup_v(t)
                 regroup_s(t)
                 if t + XBUFS < B:
                     load_x(t + XBUFS)
-            if t in chunk_at:
-                maxes(chunk_at[t])
-            if t == -3:
-                nc.vector.tensor_scalar(
-                    out=c2dup[:],
-                    in0=c2raw[:].unsqueeze(2).to_broadcast([P, PACK, 2, K]),
-                    scalar1=-1.0,
-                    scalar2=None,
-                    op0=ALU.mult,
-                )
-                c2ps = ps_tr.tile([P, PACK, P], F32, name="trps")
-                for ch in range(PACK):
-                    nc.tensor.transpose(
-                        c2ps[:, ch, :], c2dup[:, ch, :, :].rearrange("p b k -> p (b k)"), ident[:]
-                    )
-            at(t, 1, soft_b)
             if 0 <= t - 1 < B:
                 quant_x(t - 1)
-            if t == 1:
-                nc.vector.tensor_copy(out=negc2t[:], in_=c2ps[:])
-            at(t, 2, acopy)
-            pe = (t + 2) // 2
-            if 0 <= pe < NPAIR:
-                exps(pe, (t + 2) % 2)
+            if t in (1, 3, 5, 7):
+                a_sum(4 + (t - 1) // 2)
+            if t == 2:
+                acopy(0)
+            if t == 10:
+                acopy(1)
             at(t, 3, stt)
+            at(t, 6, rtotal)
             at(t, 4, square)
-            at(t, 5, total)
-            at(t, 0, soft_a)
-            at(t, 5, scale)
             at(t, 6, finish)
+            at(t, 4, rnorm)
+            at(t, 5, total)
+            at(t, 5, scale)

@@ -21,6 +21,7 @@ PASSES = N // (P * PACK)
 NPAIR = B // 2
 XBUFS = 8
 NV = [224, 288] + [576] * 13 + [512]
+INLINE = 4
 ZCHUNKS = [(0, 1), (1, 2), (2, 4), (4, 6), (6, 8)]
 
 FLOPS = 2 * B * N * K * D
@@ -37,6 +38,7 @@ def tile_modelnew_kernel(tc, x, bn_out, clusters2, out):
         mpool = ctx.enter_context(tc.tile_pool(name="maxes", bufs=2))
         epool = ctx.enter_context(tc.tile_pool(name="epi", bufs=3))
         tiny = ctx.enter_context(tc.tile_pool(name="tiny", bufs=4))
+        opool = ctx.enter_context(tc.tile_pool(name="outs", bufs=5))
         keep = ctx.enter_context(tc.tile_pool(name="keep", bufs=NPAIR))
         ps_acc = ctx.enter_context(tc.psum_pool(name="ps_acc", bufs=2))
         ps_tr = ctx.enter_context(tc.psum_pool(name="ps_tr", bufs=2))
@@ -127,16 +129,18 @@ def tile_modelnew_kernel(tc, x, bn_out, clusters2, out):
             nc.vector.reciprocal(out=rinvs[pr][:], in_=sumss[pr][:])
             pgs[pr] = spool.tile([P, 2, PASSES, K, PACK], BF16, name="pg", align_bytes=64)
 
+        def a_sum_step(pr, i):
+            nc.tensor.matmul(
+                out=asps[pr // 4][:, pr % 4, :],
+                lhsT=es[pr][:, i // PACK, i % PACK, :, :].rearrange("p b k -> p (b k)"),
+                rhs=rinvs[pr][:, i // PACK, i % PACK, :],
+                start=(i == 0),
+                stop=(i == PASSES * PACK - 1),
+            )
+
         def a_sum(pr):
-            for c in range(PASSES):
-                for j in range(PACK):
-                    nc.tensor.matmul(
-                        out=asps[pr // 4][:, pr % 4, :],
-                        lhsT=es[pr][:, c, j, :, :].rearrange("p b k -> p (b k)"),
-                        rhs=rinvs[pr][:, c, j, :],
-                        start=(c == 0 and j == 0),
-                        stop=(c == PASSES - 1 and j == PACK - 1),
-                    )
+            for i in range(PASSES * PACK):
+                a_sum_step(pr, i)
 
         def acopy(half):
             for b2 in range(2):
@@ -209,7 +213,7 @@ def tile_modelnew_kernel(tc, x, bn_out, clusters2, out):
                 )
 
         def stt(pr):
-            v = epool.tile([P, PACK, P], F32, name="v")
+            v = keep.tile([P, PACK, P], F32, name="v", tag="e")
             nc.vector.scalar_tensor_tensor(
                 out=v[:],
                 in0=negc2t[:],
@@ -249,13 +253,22 @@ def tile_modelnew_kernel(tc, x, bn_out, clusters2, out):
             )
             st[pr]["totps"] = totps
 
-        def scale(pr):
+        def scale(pr, on_vector=False, bank=None):
             vs = epool.tile([P, PACK, P], F32, name="vs")
-            nc.scalar.activation(out=vs[:], in_=st[pr]["v"][:], func=ACT.Copy, scale=st[pr]["rn"][:, 0:1])
-            trps = ps_tr.tile([P, PACK, P], F32, name="trps")
+            if on_vector:
+                nc.vector.tensor_scalar(
+                    out=vs[:], in0=st[pr]["v"][:], scalar1=st[pr]["rn"][:, 0:1], scalar2=None, op0=ALU.mult
+                )
+            else:
+                nc.scalar.activation(out=vs[:], in_=st[pr]["v"][:], func=ACT.Copy, scale=st[pr]["rn"][:, 0:1])
+            if bank is None:
+                trps = ps_tr.tile([P, PACK, P], F32, name="trps")
+            else:
+                trps = ps_as.tile([P, PACK, P], F32, name="trps_late", tag=bank)
             for ch in range(PACK):
                 nc.tensor.transpose(trps[:, ch, :], vs[:, ch, :], ident[:])
             st[pr]["trps"] = trps
+            st[pr]["o"] = opool.tile([P, 2, PACK, K], F32, name="o")
 
         def rtotal(pr):
             r2 = tiny.tile([P, 2], F32, name="r2")
@@ -264,20 +277,24 @@ def tile_modelnew_kernel(tc, x, bn_out, clusters2, out):
             )
             st[pr]["r2"] = r2
 
-        def finish(pr):
-            r2 = st[pr]["r2"]
-            o = epool.tile([P, 2, PACK, K], F32, name="o")
-            for b2 in range(2):
-                nc.scalar.activation(
-                    out=o[:, b2],
-                    in_=st[pr]["trps"][:, :, K * b2 : K * b2 + K],
-                    func=ACT.Copy,
-                    scale=r2[:, b2 : b2 + 1],
-                )
-            nc.scalar.dma_start(
+        def finish_half(pr, b2, on_vector=False):
+            src = st[pr]["trps"][:, :, K * b2 : K * b2 + K]
+            r2 = st[pr]["r2"][:, b2 : b2 + 1]
+            if on_vector:
+                nc.vector.tensor_scalar(out=st[pr]["o"][:, b2], in0=src, scalar1=r2, scalar2=None, op0=ALU.mult)
+            else:
+                nc.scalar.activation(out=st[pr]["o"][:, b2], in_=src, func=ACT.Copy, scale=r2)
+
+        def store(pr):
+            nc.sync.dma_start(
                 out=out[2 * pr : 2 * pr + 2, :].rearrange("b (q r) -> q b r", q=P),
-                in_=o[:].rearrange("p b c k -> p b (c k)"),
+                in_=st[pr]["o"][:].rearrange("p b c k -> p b (c k)"),
             )
+
+        def finish(pr, on_vector=False):
+            finish_half(pr, 0, on_vector)
+            finish_half(pr, 1, on_vector)
+            store(pr)
 
         load_z(0)
         load_z(1)
@@ -348,28 +365,47 @@ def tile_modelnew_kernel(tc, x, bn_out, clusters2, out):
         for i in range(4):
             quant_p(NPAIR - 1, i)
 
-        def at(t, lag, step):
-            if (t - lag) % 2 == 0 and 0 <= (t - lag) // 2 < NPAIR:
+        def at(t, lag, step, end):
+            if (t - lag) % 2 == 0 and 0 <= (t - lag) // 2 < end:
                 step((t - lag) // 2)
 
-        for t in range(B + 7):
+        for t in range(B + 1):
             if t < B:
                 regroup_v(t)
                 regroup_s(t)
                 if t + XBUFS < B:
                     load_x(t + XBUFS)
-            if 0 <= t - 1 < B:
+            if t >= 1:
                 quant_x(t - 1)
-            if t in (1, 3, 5, 7):
-                a_sum(4 + (t - 1) // 2)
+            if t < 8:
+                for i in range(4 * t, 4 * t + 4):
+                    a_sum_step(4 + i // 8, i % 8)
             if t == 2:
                 acopy(0)
             if t == 10:
                 acopy(1)
-            at(t, 3, stt)
-            at(t, 6, rtotal)
-            at(t, 4, square)
-            at(t, 6, finish)
-            at(t, 4, rnorm)
-            at(t, 5, total)
-            at(t, 5, scale)
+            at(t, 3, stt, 7)
+            at(t, 6, rtotal, 6)
+            at(t, 4, square, 7)
+            at(t, 6, finish, INLINE)
+            at(t, 4, rnorm, 7)
+            at(t, 5, total, 6)
+            at(t, 5, scale, INLINE)
+
+        scale(4)
+        scale(5)
+        total(6)
+        scale(6, on_vector=True, bank="asps0")
+        stt(7)
+        square(7)
+        finish(5, on_vector=True)
+        rnorm(7)
+        finish(4)
+        total(7)
+        scale(7, on_vector=True, bank="asps1")
+        rtotal(6)
+        finish(6)
+        rtotal(7)
+        finish_half(7, 0)
+        finish_half(7, 1, on_vector=True)
+        store(7)

@@ -20,7 +20,7 @@ PACK = 4
 PASSES = N // (P * PACK)
 NPAIR = B // 2
 XBUFS = 8
-NV = [224, 288] + [576] * 13 + [512]
+NV = [224, 288] + [512] * 14
 INLINE = 4
 ZCHUNKS = [(0, 1), (1, 2), (2, 4), (4, 6), (6, 8)]
 
@@ -253,14 +253,11 @@ def tile_modelnew_kernel(tc, x, bn_out, clusters2, out):
             )
             st[pr]["totps"] = totps
 
-        def scale(pr, on_vector=False, bank=None):
+        def scale(pr, bank=None):
             vs = epool.tile([P, PACK, P], F32, name="vs")
-            if on_vector:
-                nc.vector.tensor_scalar(
-                    out=vs[:], in0=st[pr]["v"][:], scalar1=st[pr]["rn"][:, 0:1], scalar2=None, op0=ALU.mult
-                )
-            else:
-                nc.scalar.activation(out=vs[:], in_=st[pr]["v"][:], func=ACT.Copy, scale=st[pr]["rn"][:, 0:1])
+            nc.vector.tensor_scalar(
+                out=vs[:], in0=st[pr]["v"][:], scalar1=st[pr]["rn"][:, 0:1], scalar2=None, op0=ALU.mult
+            )
             if bank is None:
                 trps = ps_tr.tile([P, PACK, P], F32, name="trps")
             else:
@@ -395,14 +392,14 @@ def tile_modelnew_kernel(tc, x, bn_out, clusters2, out):
         scale(4)
         scale(5)
         total(6)
-        scale(6, on_vector=True, bank="asps0")
+        scale(6, bank="asps0")
         stt(7)
         square(7)
         finish(5, on_vector=True)
         rnorm(7)
         finish(4)
         total(7)
-        scale(7, on_vector=True, bank="asps1")
+        scale(7, bank="asps1")
         rtotal(6)
         finish(6)
         rtotal(7)

@@ -74,7 +74,7 @@ def tile_modelnew_kernel(tc, x, bn_out, clusters2, out):
         eps_t = const.tile([P, 1], F32)
         c2raw = const.tile([P, PACK, K], BF16)
         c2dup = const.tile([P, PACK, 2, K], F32)
-        negc2t = const.tile([P, PACK, P], F32)
+        c2t = const.tile([P, PACK, P], F32)
 
         zview = bn_out.rearrange("(s p j) k -> p s (j k)", p=P, j=PACK)
 
@@ -127,7 +127,7 @@ def tile_modelnew_kernel(tc, x, bn_out, clusters2, out):
 
         def recip(pr):
             nc.vector.reciprocal(out=rinvs[pr][:], in_=sumss[pr][:])
-            pgs[pr] = spool.tile([P, 2, PASSES, K, PACK], BF16, name="pg", align_bytes=64)
+            pgs[pr] = spool.tile([P, PASSES, 2, K, PACK], BF16, name="pg", align_bytes=64)
 
         def a_sum_step(pr, i):
             nc.tensor.matmul(
@@ -144,14 +144,17 @@ def tile_modelnew_kernel(tc, x, bn_out, clusters2, out):
 
         def acopy(half):
             for b2 in range(2):
-                nc.vector.tensor_copy(
+                nc.vector.tensor_scalar(
                     out=asum[64 * b2 : 64 * b2 + 64, 4 * half : 4 * half + 4],
-                    in_=asps[half][64 * b2 : 64 * b2 + 64, :, b2],
+                    in0=asps[half][64 * b2 : 64 * b2 + 64, :, b2],
+                    scalar1=-1.0,
+                    scalar2=None,
+                    op0=ALU.mult,
                 )
 
         def norm(pr, b2):
             nc.vector.tensor_tensor(
-                out=pgs[pr][:, b2],
+                out=pgs[pr][:, :, b2],
                 in0=es[pr][:, :, :, b2, :].rearrange("p c j k -> p c k j"),
                 in1=rinvs[pr][:, :, :, b2].unsqueeze(2).to_broadcast([P, PASSES, K, PACK]),
                 op=ALU.mult,
@@ -160,12 +163,13 @@ def tile_modelnew_kernel(tc, x, bn_out, clusters2, out):
         def quant_p(pr, i):
             if pr < 0:
                 return
-            b2 = i // PASSES
-            c = i % PASSES
+            g0, g1 = ((0, 1), (1, 3), (3, 4))[i]
+            w0 = (0, 128, 320)[i]
+            w1 = w0 + K * (g1 - g0)
             nc.vector.quantize_mx(
-                out=pws[pr][:, c, 128 * b2 : 128 * b2 + K].bitcast(FP8X4),
-                scales=pscales[pr][:, c, 128 * b2 : 128 * b2 + K],
-                in_=pgs[pr][:, b2, c, :, :].rearrange("p k j -> p (k j)"),
+                out=pws[pr][:].rearrange("p c w -> p (c w)")[:, w0:w1].bitcast(FP8X4),
+                scales=pscales[pr][:].rearrange("p c w -> p (c w)")[:, w0:w1],
+                in_=pgs[pr][:].rearrange("p c b k j -> p (c b) (k j)")[:, g0:g1, :].rearrange("p g f -> p (g f)"),
             )
 
         groupeds = {}
@@ -216,7 +220,7 @@ def tile_modelnew_kernel(tc, x, bn_out, clusters2, out):
             v = keep.tile([P, PACK, P], F32, name="v", tag="e")
             nc.vector.scalar_tensor_tensor(
                 out=v[:],
-                in0=negc2t[:],
+                in0=c2t[:],
                 scalar=asum[:, pr : pr + 1],
                 in1=st[pr]["acc"][:].rearrange("p (q c) -> p c q", c=PACK),
                 op0=ALU.mult,
@@ -293,12 +297,12 @@ def tile_modelnew_kernel(tc, x, bn_out, clusters2, out):
             finish_half(pr, 1, on_vector)
             store(pr)
 
-        load_z(0)
-        load_z(1)
         nc.sync.dma_start(
             out=c2raw[:].rearrange("p c k -> p (c k)"),
             in_=clusters2[0].rearrange("(q c) k -> q (c k)", c=PACK),
         )
+        load_z(0)
+        load_z(1)
         load_z(2)
         load_z(3)
         load_z(4)
@@ -314,24 +318,15 @@ def tile_modelnew_kernel(tc, x, bn_out, clusters2, out):
         nc.gpsimd.memset(mask[64:128, 1:2], 1.0)
         nc.gpsimd.memset(eps_t[:], EPS)
 
-        for step in max_steps(0):
-            step()
-        exps(0)
-        m1 = max_steps(1)
-        m1[0]()
-        nc.vector.tensor_scalar(
-            out=c2dup[:],
-            in0=c2raw[:].unsqueeze(2).to_broadcast([P, PACK, 2, K]),
-            scalar1=-1.0,
-            scalar2=None,
-            op0=ALU.mult,
-        )
+        nc.scalar.copy(out=c2dup[:], in_=c2raw[:].unsqueeze(2).to_broadcast([P, PACK, 2, K]))
         c2ps = ps_tr.tile([P, PACK, P], F32, name="trps")
         for ch in range(PACK):
             nc.tensor.transpose(c2ps[:, ch, :], c2dup[:, ch, :, :].rearrange("p b k -> p (b k)"), ident[:])
-        m1[1]()
-        m1[2]()
-        m1[3]()
+        for step in max_steps(0):
+            step()
+        exps(0)
+        for step in max_steps(1):
+            step()
         exps(1)
         for step in max_steps(2):
             step()
@@ -353,13 +348,12 @@ def tile_modelnew_kernel(tc, x, bn_out, clusters2, out):
             norm(pr, 1)
             quant_p(pr - 1, 2)
             one_max(4 * pr + 2)
-            quant_p(pr - 1, 3)
-            one_max(4 * pr + 3)
             if pr == 0:
-                nc.vector.tensor_copy(out=negc2t[:], in_=c2ps[:])
+                nc.vector.tensor_copy(out=c2t[:], in_=c2ps[:])
+            one_max(4 * pr + 3)
             if pr + 2 < NPAIR:
                 exps(pr + 2)
-        for i in range(4):
+        for i in range(3):
             quant_p(NPAIR - 1, i)
 
         def at(t, lag, step, end):

@@ -22,7 +22,7 @@ NPAIR = B // 2
 XBUFS = 8
 NV = [224, 288] + [512] * 14
 INLINE = 4
-ZCHUNKS = [(0, 1), (1, 2), (2, 4), (4, 6), (6, 8)]
+ZCHUNKS = [(0, 1), (1, 2), (2, 4), (4, 8)]
 
 FLOPS = 2 * B * N * K * D
 
@@ -34,8 +34,7 @@ def tile_modelnew_kernel(tc, x, bn_out, clusters2, out):
         xpool = ctx.enter_context(tc.tile_pool(name="xraw", bufs=XBUFS))
         gpool = ctx.enter_context(tc.tile_pool(name="grouped", bufs=4))
         wpool = ctx.enter_context(tc.tile_pool(name="xwords", bufs=4))
-        spool = ctx.enter_context(tc.tile_pool(name="soft", bufs=3))
-        mpool = ctx.enter_context(tc.tile_pool(name="maxes", bufs=2))
+        mpool = ctx.enter_context(tc.tile_pool(name="maxes", bufs=1))
         epool = ctx.enter_context(tc.tile_pool(name="epi", bufs=3))
         tiny = ctx.enter_context(tc.tile_pool(name="tiny", bufs=4))
         opool = ctx.enter_context(tc.tile_pool(name="outs", bufs=5))
@@ -59,14 +58,13 @@ def tile_modelnew_kernel(tc, x, bn_out, clusters2, out):
         es = []
         sumss = []
         rinvs = []
-        pws = []
-        pscales = []
         for pr in range(NPAIR):
-            es.append(keep.tile([P, PASSES, PACK, 2, K], F32, name="e"))
-            sumss.append(keep.tile([P, PASSES, PACK, 2], F32, name="sums"))
-            rinvs.append(keep.tile([P, PASSES, PACK, 2], F32, name="rinv"))
-            pws.append(keep.tile([P, PASSES, 192], U32, name="pw", align_bytes=64))
-            pscales.append(keep.tile([P, PASSES, 192], U8, name="pscale", align_bytes=64))
+            es.append(keep.tile([P, PACK, PASSES, 2, K], F32, name="e"))
+            sumss.append(keep.tile([P, PACK, PASSES, 2], F32, name="sums"))
+            rinvs.append(keep.tile([P, PACK, PASSES, 2], F32, name="rinv"))
+        pg = const.tile([P, NPAIR * PASSES * 2, K, PACK], BF16, align_bytes=64)
+        pw = const.tile([P, NPAIR, PASSES, 192], U32, align_bytes=64)
+        pscale = const.tile([P, NPAIR, PASSES, 192], U8, align_bytes=64)
         asum = const.tile([P, NPAIR], F32)
         asps = [ps_as.tile([P, 4, 2], F32, name="asps0"), ps_as.tile([P, 4, 2], F32, name="asps1")]
         ident = const.tile([P, P], F32)
@@ -78,10 +76,14 @@ def tile_modelnew_kernel(tc, x, bn_out, clusters2, out):
 
         zview = bn_out.rearrange("(s p j) k -> p s (j k)", p=P, j=PACK)
 
-        def load_z(ch):
+        def load_z(ch, first=0, end=None):
             s0 = ZCHUNKS[ch][0] * 2 * PASSES
             s1 = ZCHUNKS[ch][1] * 2 * PASSES
-            nc.sync.dma_start(out=zts[ch][:].rearrange("p s j k -> p s (j k)"), in_=zview[:, s0:s1, :])
+            if end is None:
+                end = s1 - s0
+            nc.sync.dma_start(
+                out=zts[ch][:, first:end, :, :].rearrange("p s j k -> p s (j k)"), in_=zview[:, s0 + first : s0 + end, :]
+            )
 
         xraw = {}
 
@@ -95,9 +97,9 @@ def tile_modelnew_kernel(tc, x, bn_out, clusters2, out):
         def max_steps(ch):
             ns = (ZCHUNKS[ch][1] - ZCHUNKS[ch][0]) * 2 * PASSES * PACK
             zc = zts[ch][:].rearrange("p s j k -> p (s j) k")
-            t1 = mpool.tile([P, ns, 32], BF16, name="t1")
-            t2 = mpool.tile([P, ns, 16], BF16, name="t2")
-            t3 = mpool.tile([P, ns, 8], BF16, name="t3")
+            t1 = mpool.tile([P, ns, 32], BF16, name="t1_%d" % ch)
+            t2 = mpool.tile([P, ns, 16], BF16, name="t2_%d" % ch)
+            t3 = mpool.tile([P, ns, 8], BF16, name="t3_%d" % ch)
             return [
                 lambda: nc.vector.tensor_tensor(out=t1[:], in0=zc[:, :, 0:32], in1=zc[:, :, 32:64], op=ALU.max),
                 lambda: nc.vector.tensor_tensor(out=t2[:], in0=t1[:, :, 0:16], in1=t1[:, :, 16:32], op=ALU.max),
@@ -107,6 +109,11 @@ def tile_modelnew_kernel(tc, x, bn_out, clusters2, out):
                 ),
             ]
 
+        def first_max(s):
+            nc.vector.tensor_reduce(
+                out=negmaxes[0][:, PACK * s : PACK * s + PACK], in_=zts[0][:, s, :, :], axis=AX.X, op=ALU.max, negate=True
+            )
+
         def exps(pr):
             ch = chunk_of[pr]
             for b2 in range(2):
@@ -115,25 +122,22 @@ def tile_modelnew_kernel(tc, x, bn_out, clusters2, out):
                     for j in range(PACK):
                         i = s * PACK + j
                         nc.scalar.activation(
-                            out=es[pr][:, c, j, b2, :],
+                            out=es[pr][:, j, c, b2, :],
                             in_=zts[ch][:, s, j, :],
                             func=ACT.Exp,
                             bias=negmaxes[ch][:, i : i + 1],
                             scale=1.0,
-                            accum_out=sumss[pr][:, c, j, b2 : b2 + 1],
+                            accum_out=sumss[pr][:, j, c, b2 : b2 + 1],
                         )
-
-        pgs = {}
 
         def recip(pr):
             nc.vector.reciprocal(out=rinvs[pr][:], in_=sumss[pr][:])
-            pgs[pr] = spool.tile([P, PASSES, 2, K, PACK], BF16, name="pg", align_bytes=64)
 
         def a_sum_step(pr, i):
             nc.tensor.matmul(
                 out=asps[pr // 4][:, pr % 4, :],
-                lhsT=es[pr][:, i // PACK, i % PACK, :, :].rearrange("p b k -> p (b k)"),
-                rhs=rinvs[pr][:, i // PACK, i % PACK, :],
+                lhsT=es[pr][:, i // PASSES, i % PASSES, :, :].rearrange("p b k -> p (b k)"),
+                rhs=rinvs[pr][:, i // PASSES, i % PASSES, :],
                 start=(i == 0),
                 stop=(i == PASSES * PACK - 1),
             )
@@ -152,25 +156,28 @@ def tile_modelnew_kernel(tc, x, bn_out, clusters2, out):
                     op0=ALU.mult,
                 )
 
-        def norm(pr, b2):
+        def norm(pr):
             nc.vector.tensor_tensor(
-                out=pgs[pr][:, :, b2],
-                in0=es[pr][:, :, :, b2, :].rearrange("p c j k -> p c k j"),
-                in1=rinvs[pr][:, :, :, b2].unsqueeze(2).to_broadcast([P, PASSES, K, PACK]),
+                out=pg[:, 4 * pr : 4 * pr + 4, :, :],
+                in0=es[pr][:].rearrange("p j c b k -> p (c b) k j"),
+                in1=rinvs[pr][:].rearrange("p j c b -> p (c b) j").unsqueeze(2).to_broadcast([P, 4, K, PACK]),
                 op=ALU.mult,
             )
 
-        def quant_p(pr, i):
-            if pr < 0:
-                return
-            g0, g1 = ((0, 1), (1, 3), (3, 4))[i]
-            w0 = (0, 128, 320)[i]
+        def quant_p(g0, g1):
+            w0 = 384 * (g0 // 4) + 192 * ((g0 % 4) // 2) + 128 * (g0 % 2)
             w1 = w0 + K * (g1 - g0)
             nc.vector.quantize_mx(
-                out=pws[pr][:].rearrange("p c w -> p (c w)")[:, w0:w1].bitcast(FP8X4),
-                scales=pscales[pr][:].rearrange("p c w -> p (c w)")[:, w0:w1],
-                in_=pgs[pr][:].rearrange("p c b k j -> p (c b) (k j)")[:, g0:g1, :].rearrange("p g f -> p (g f)"),
+                out=pw[:].rearrange("p r c w -> p (r c w)")[:, w0:w1].bitcast(FP8X4),
+                scales=pscale[:].rearrange("p r c w -> p (r c w)")[:, w0:w1],
+                in_=pg[:, g0:g1, :, :].rearrange("p g k j -> p (g k j)"),
             )
+
+        def quant_p_pair(pr):
+            if pr < 0:
+                return
+            quant_p(max(4 * pr - 1, 0), 4 * pr + 1)
+            quant_p(4 * pr + 1, 4 * pr + 3)
 
         groupeds = {}
 
@@ -199,17 +206,17 @@ def tile_modelnew_kernel(tc, x, bn_out, clusters2, out):
             xs = wpool.tile([P, PASSES, D], U8, name="xs", align_bytes=64)
             if b2 == 0:
                 st[pr] = {"acc": ps_acc.tile([P, D], F32, name="acc")}
-            for c in range(PASSES):
+            for c0, c1 in ((0, 1), (1, 2)) if b == B - 1 else ((0, 2),):
                 nc.vector.quantize_mx(
-                    out=xw[:, c, :].bitcast(FP8X4),
-                    scales=xs[:, c, :],
-                    in_=groupeds[b][:, c, :, :].rearrange("p d t -> p (d t)"),
+                    out=xw[:, c0:c1, :].rearrange("p c d -> p (c d)").bitcast(FP8X4),
+                    scales=xs[:, c0:c1, :].rearrange("p c d -> p (c d)"),
+                    in_=groupeds[b][:, c0:c1, :, :].rearrange("p c d t -> p (c d t)"),
                 )
             for c in range(PASSES):
                 nc.tensor.matmul_mx(
                     out=st[pr]["acc"][:],
-                    lhsT=pws[pr][:, c, 64 * b2 : 64 * b2 + P].bitcast(FP8X4),
-                    lhsT_scale=pscales[pr][:, c, 64 * b2 : 64 * b2 + P],
+                    lhsT=pw[:, pr, c, 64 * b2 : 64 * b2 + P].bitcast(FP8X4),
+                    lhsT_scale=pscale[:, pr, c, 64 * b2 : 64 * b2 + P],
                     rhs=xw[:, c, :].bitcast(FP8X4),
                     rhs_scale=xs[:, c, :],
                     start=(b2 == 0 and c == 0),
@@ -301,17 +308,15 @@ def tile_modelnew_kernel(tc, x, bn_out, clusters2, out):
             out=c2raw[:].rearrange("p c k -> p (c k)"),
             in_=clusters2[0].rearrange("(q c) k -> q (c k)", c=PACK),
         )
-        load_z(0)
-        load_z(1)
-        load_z(2)
-        load_z(3)
-        load_z(4)
+        load_z(0, 0, 1)
+        load_z(0, 1, 2 * PASSES)
+        for ch in range(1, len(ZCHUNKS)):
+            load_z(ch)
         for b in range(XBUFS):
             load_x(b)
 
-        for pr in range(NPAIR):
-            nc.vector.memset(pws[pr][:, :, 64:128].bitcast(I32), 0)
-            nc.vector.memset(pscales[pr][:, :, 64:128].bitcast(I32), 0)
+        nc.vector.memset(pw[:, :, :, 64:128].bitcast(I32), 0)
+        nc.vector.memset(pscale[:, :, :, 64:128].bitcast(I32), 0)
         make_identity(nc, ident[:])
         nc.gpsimd.memset(mask[:], 0.0)
         nc.gpsimd.memset(mask[0:64, 0:1], 1.0)
@@ -322,39 +327,29 @@ def tile_modelnew_kernel(tc, x, bn_out, clusters2, out):
         c2ps = ps_tr.tile([P, PACK, P], F32, name="trps")
         for ch in range(PACK):
             nc.tensor.transpose(c2ps[:, ch, :], c2dup[:, ch, :, :].rearrange("p b k -> p (b k)"), ident[:])
-        for step in max_steps(0):
-            step()
+        for s in range(2 * PASSES):
+            first_max(s)
         exps(0)
         for step in max_steps(1):
             step()
         exps(1)
         for step in max_steps(2):
             step()
-        later = max_steps(3) + max_steps(4)
-
-        def one_max(i):
-            if i < len(later):
-                later[i]()
-
         for pr in range(NPAIR):
             recip(pr)
             if pr < 4:
                 a_sum(pr)
-            quant_p(pr - 1, 0)
-            one_max(4 * pr)
-            norm(pr, 0)
-            quant_p(pr - 1, 1)
-            one_max(4 * pr + 1)
-            norm(pr, 1)
-            quant_p(pr - 1, 2)
-            one_max(4 * pr + 2)
+            quant_p_pair(pr - 1)
             if pr == 0:
                 nc.vector.tensor_copy(out=c2t[:], in_=c2ps[:])
-            one_max(4 * pr + 3)
+            norm(pr)
+            if pr == 0:
+                for step in max_steps(3):
+                    step()
             if pr + 2 < NPAIR:
                 exps(pr + 2)
-        for i in range(3):
-            quant_p(NPAIR - 1, i)
+        quant_p_pair(NPAIR - 1)
+        quant_p(4 * NPAIR - 1, 4 * NPAIR)
 
         def at(t, lag, step, end):
             if (t - lag) % 2 == 0 and 0 <= (t - lag) // 2 < end:
@@ -376,22 +371,23 @@ def tile_modelnew_kernel(tc, x, bn_out, clusters2, out):
             if t == 10:
                 acopy(1)
             at(t, 3, stt, 7)
-            at(t, 6, rtotal, 6)
+            at(t, 6, rtotal, 5)
             at(t, 4, square, 7)
             at(t, 6, finish, INLINE)
             at(t, 4, rnorm, 7)
             at(t, 5, total, 6)
-            at(t, 5, scale, INLINE)
+            at(t, 5, scale, 6)
 
-        scale(4)
-        scale(5)
+        finish(4)
+        rtotal(5)
+        stt(7)
+        finish_half(5, 0)
+        square(7)
         total(6)
         scale(6, bank="asps0")
-        stt(7)
-        square(7)
-        finish(5, on_vector=True)
         rnorm(7)
-        finish(4)
+        finish_half(5, 1)
+        store(5)
         total(7)
         scale(7, bank="asps1")
         rtotal(6)

@@ -61,7 +61,7 @@ def tile_modelnew_kernel(tc, x, bn_out, clusters2, out):
         for pr in range(NPAIR):
             es.append(keep.tile([P, PACK, PASSES, 2, K], F32, name="e"))
             sumss.append(keep.tile([P, PACK, PASSES, 2], F32, name="sums"))
-            rinvs.append(keep.tile([P, PACK, PASSES, 2], F32, name="rinv"))
+            rinvs.append(keep.tile([P, PACK, PASSES, 2, 2], F32, name="rinv"))
         pg = const.tile([P, NPAIR * PASSES * 2, K, PACK], BF16, align_bytes=64)
         pw = const.tile([P, NPAIR, PASSES, 192], U32, align_bytes=64)
         pscale = const.tile([P, NPAIR, PASSES, 192], U8, align_bytes=64)
@@ -131,13 +131,13 @@ def tile_modelnew_kernel(tc, x, bn_out, clusters2, out):
                         )
 
         def recip(pr):
-            nc.vector.reciprocal(out=rinvs[pr][:], in_=sumss[pr][:])
+            nc.vector.reciprocal(out=rinvs[pr][:], in_=sumss[pr][:].unsqueeze(4).to_broadcast([P, PACK, PASSES, 2, 2]))
 
         def a_sum_step(pr, i):
             nc.tensor.matmul(
                 out=asps[pr // 4][:, pr % 4, :],
                 lhsT=es[pr][:, i // PASSES, i % PASSES, :, :].rearrange("p b k -> p (b k)"),
-                rhs=rinvs[pr][:, i // PASSES, i % PASSES, :],
+                rhs=rinvs[pr][:, i // PASSES, i % PASSES, :, 0],
                 start=(i == 0),
                 stop=(i == PASSES * PACK - 1),
             )
@@ -157,12 +157,14 @@ def tile_modelnew_kernel(tc, x, bn_out, clusters2, out):
                 )
 
         def norm(pr):
-            nc.vector.tensor_tensor(
-                out=pg[:, 4 * pr : 4 * pr + 4, :, :],
-                in0=es[pr][:].rearrange("p j c b k -> p (c b) k j"),
-                in1=rinvs[pr][:].rearrange("p j c b -> p (c b) j").unsqueeze(2).to_broadcast([P, 4, K, PACK]),
-                op=ALU.mult,
-            )
+            for c in range(PASSES):
+                for b2 in range(2):
+                    nc.vector.tensor_tensor(
+                        out=pg[:, 4 * pr + 2 * c + b2, :, :].rearrange("p (w i) j -> p w j i", i=2),
+                        in0=es[pr][:, :, c, b2, :].rearrange("p j (w i) -> p w j i", i=2),
+                        in1=rinvs[pr][:, :, c, b2, :].unsqueeze(1).to_broadcast([P, K // 2, PACK, 2]),
+                        op=ALU.mult,
+                    )
 
         def quant_p(g0, g1):
             w0 = 384 * (g0 // 4) + 192 * ((g0 % 4) // 2) + 128 * (g0 % 2)

@@ -365,8 +365,8 @@ def tile_modelnew_kernel(tc, x, bn_out, clusters2, out):
                     load_x(t + XBUFS)
             if t >= 1:
                 quant_x(t - 1)
-            if t < 8:
-                for i in range(4 * t, 4 * t + 4):
+            if 2 <= t < 10:
+                for i in range(4 * (t - 2), 4 * (t - 2) + 4):
                     a_sum_step(4 + i // 8, i % 8)
             if t == 2:
                 acopy(0)

@@ -60,8 +60,8 @@ def tile_modelnew_kernel(tc, x, bn_out, clusters2, out):
         rinvs = []
         for pr in range(NPAIR):
             es.append(keep.tile([P, PACK, PASSES, 2, K], F32, name="e"))
-            sumss.append(keep.tile([P, PACK, PASSES, 2], F32, name="sums"))
-            rinvs.append(keep.tile([P, PACK, PASSES, 2, 2], F32, name="rinv"))
+            sumss.append(keep.tile([P, PASSES, 2, PACK], F32, name="sums"))
+            rinvs.append(keep.tile([P, PASSES, 2, PACK], F32, name="rinv"))
         pg = const.tile([P, NPAIR * PASSES * 2, K, PACK], BF16, align_bytes=64)
         pw = const.tile([P, NPAIR, PASSES, 192], U32, align_bytes=64)
         pscale = const.tile([P, NPAIR, PASSES, 192], U8, align_bytes=64)
@@ -127,17 +127,17 @@ def tile_modelnew_kernel(tc, x, bn_out, clusters2, out):
                             func=ACT.Exp,
                             bias=negmaxes[ch][:, i : i + 1],
                             scale=1.0,
-                            accum_out=sumss[pr][:, j, c, b2 : b2 + 1],
+                            accum_out=sumss[pr][:, c, b2, j : j + 1],
                         )
 
         def recip(pr):
-            nc.vector.reciprocal(out=rinvs[pr][:], in_=sumss[pr][:].unsqueeze(4).to_broadcast([P, PACK, PASSES, 2, 2]))
+            nc.vector.reciprocal(out=rinvs[pr][:], in_=sumss[pr][:])
 
         def a_sum_step(pr, i):
             nc.tensor.matmul(
                 out=asps[pr // 4][:, pr % 4, :],
                 lhsT=es[pr][:, i // PASSES, i % PASSES, :, :].rearrange("p b k -> p (b k)"),
-                rhs=rinvs[pr][:, i // PASSES, i % PASSES, :, 0],
+                rhs=rinvs[pr][:, i % PASSES, :, i // PASSES],
                 start=(i == 0),
                 stop=(i == PASSES * PACK - 1),
             )
@@ -162,7 +162,7 @@ def tile_modelnew_kernel(tc, x, bn_out, clusters2, out):
                     nc.vector.tensor_tensor(
                         out=pg[:, 4 * pr + 2 * c + b2, :, :].rearrange("p (w i) j -> p w j i", i=2),
                         in0=es[pr][:, :, c, b2, :].rearrange("p j (w i) -> p w j i", i=2),
-                        in1=rinvs[pr][:, :, c, b2, :].unsqueeze(1).to_broadcast([P, K // 2, PACK, 2]),
+                        in1=rinvs[pr][:, c, b2, :].unsqueeze(1).unsqueeze(3).to_broadcast([P, K // 2, PACK, 2]),
                         op=ALU.mult,
                     )
 

@@ -156,9 +156,8 @@ def tile_modelnew_kernel(tc, x, bn_out, clusters2, out):
                     op0=ALU.mult,
                 )
 
-        def norm(pr):
-            for c in range(PASSES):
-                for b2 in range(2):
+        def norm(pr, parts=None):
+            for c, b2 in parts or [(0, 0), (0, 1), (1, 0), (1, 1)]:
                     nc.vector.tensor_tensor(
                         out=pg[:, 4 * pr + 2 * c + b2, :, :].rearrange("p (w i) j -> p w j i", i=2),
                         in0=es[pr][:, :, c, b2, :].rearrange("p j (w i) -> p w j i", i=2),
@@ -329,25 +328,44 @@ def tile_modelnew_kernel(tc, x, bn_out, clusters2, out):
         c2ps = ps_tr.tile([P, PACK, P], F32, name="trps")
         for ch in range(PACK):
             nc.tensor.transpose(c2ps[:, ch, :], c2dup[:, ch, :, :].rearrange("p b k -> p (b k)"), ident[:])
-        for s in range(2 * PASSES):
-            first_max(s)
+        m1 = max_steps(1)
+        m2 = max_steps(2)
+        m3 = max_steps(3)
+        first_max(0)
+        first_max(1)
+        first_max(2)
+        m1[0]()
+        first_max(3)
         exps(0)
-        for step in max_steps(1):
-            step()
+        m1[1]()
+        nc.vector.tensor_copy(out=c2t[:], in_=c2ps[:])
+        m1[2]()
+        m1[3]()
         exps(1)
-        for step in max_steps(2):
-            step()
-        for pr in range(NPAIR):
+        m2[0]()
+        recip(0)
+        a_sum(0)
+        m2[1]()
+        norm(0, [(0, 0)])
+        m2[2]()
+        norm(0, [(0, 1)])
+        m2[3]()
+        exps(2)
+        norm(0, [(1, 0)])
+        m3[0]()
+        norm(0, [(1, 1)])
+        m3[1]()
+        for pr in range(1, NPAIR):
             recip(pr)
             if pr < 4:
                 a_sum(pr)
             quant_p_pair(pr - 1)
-            if pr == 0:
-                nc.vector.tensor_copy(out=c2t[:], in_=c2ps[:])
-            norm(pr)
-            if pr == 0:
-                for step in max_steps(3):
-                    step()
+            if pr == 1:
+                m3[2]()
+            norm(pr, [(0, 0), (0, 1)])
+            if pr == 1:
+                m3[3]()
+            norm(pr, [(1, 0), (1, 1)])
             if pr + 2 < NPAIR:
                 exps(pr + 2)
         quant_p_pair(NPAIR - 1)

@@ -15,6 +15,7 @@ AX = mybir.AxisListType
 
 B, N, D, K = 16, 1024, 512, 64
 EPS = 1e-12
+HALF = D // 2
 P = 128
 PACK = 4
 PASSES = N // (P * PACK)
@@ -200,41 +201,71 @@ def tile_modelnew_kernel(tc, x, bn_out, clusters2, out):
 
         st = {}
 
-        def quant_x(b):
+        def start_acc(pr):
+            if pr < NPAIR - 1:
+                st[pr] = {"width": D, "acc": [ps_acc.tile([P, D], F32, name="acc")]}
+            else:
+                st[pr] = {
+                    "width": HALF,
+                    "acc": [
+                        ps_acc.tile([P, HALF], F32, name="acc_first", tag="acc"),
+                        ps_as.tile([P, HALF], F32, name="acc_second", tag="asps0"),
+                    ]
+                }
+
+        words = {}
+
+        def quantise(b, c0, c1, d0=0, d1=D):
+            if b not in words:
+                xw = wpool.tile([P, PASSES, D], U32, name="xw", align_bytes=64)
+                xs = wpool.tile([P, PASSES, D], U8, name="xs", align_bytes=64)
+                words[b] = (xw, xs)
+            xw, xs = words[b]
+            nc.vector.quantize_mx(
+                out=xw[:].rearrange("p c d -> p (c d)")[:, c0 * D + d0 : (c1 - 1) * D + d1].bitcast(FP8X4),
+                scales=xs[:].rearrange("p c d -> p (c d)")[:, c0 * D + d0 : (c1 - 1) * D + d1],
+                in_=groupeds[b][:].rearrange("p c d t -> p (c d t)")[
+                    :, PACK * (c0 * D + d0) : PACK * ((c1 - 1) * D + d1)
+                ],
+            )
+
+        def multiply(b, c, h=0):
             pr = b // 2
             b2 = b % 2
-            xw = wpool.tile([P, PASSES, D], U32, name="xw", align_bytes=64)
-            xs = wpool.tile([P, PASSES, D], U8, name="xs", align_bytes=64)
-            if b2 == 0:
-                st[pr] = {"acc": ps_acc.tile([P, D], F32, name="acc")}
-            for c0, c1 in ((0, 1), (1, 2)) if b == B - 1 else ((0, 2),):
-                nc.vector.quantize_mx(
-                    out=xw[:, c0:c1, :].rearrange("p c d -> p (c d)").bitcast(FP8X4),
-                    scales=xs[:, c0:c1, :].rearrange("p c d -> p (c d)"),
-                    in_=groupeds[b][:, c0:c1, :, :].rearrange("p c d t -> p (c d t)"),
-                )
-            for c in range(PASSES):
-                nc.tensor.matmul_mx(
-                    out=st[pr]["acc"][:],
-                    lhsT=pw[:, pr, c, 64 * b2 : 64 * b2 + P].bitcast(FP8X4),
-                    lhsT_scale=pscale[:, pr, c, 64 * b2 : 64 * b2 + P],
-                    rhs=xw[:, c, :].bitcast(FP8X4),
-                    rhs_scale=xs[:, c, :],
-                    start=(b2 == 0 and c == 0),
-                    stop=(b2 == 1 and c == PASSES - 1),
-                )
+            xw, xs = words[b]
+            acc = st[pr]["acc"][h]
+            cols = slice(h * HALF, h * HALF + st[pr]["width"])
+            nc.tensor.matmul_mx(
+                out=acc[:],
+                lhsT=pw[:, pr, c, 64 * b2 : 64 * b2 + P].bitcast(FP8X4),
+                lhsT_scale=pscale[:, pr, c, 64 * b2 : 64 * b2 + P],
+                rhs=xw[:, c, cols].bitcast(FP8X4),
+                rhs_scale=xs[:, c, cols],
+                start=(b2 == 0 and c == 0),
+                stop=(b2 == 1 and c == PASSES - 1),
+            )
 
-        def stt(pr):
-            v = keep.tile([P, PACK, P], F32, name="v", tag="e")
+        def quant_x(b):
+            if b % 2 == 0:
+                start_acc(b // 2)
+            quantise(b, 0, PASSES)
+            for c in range(PASSES):
+                for h in range(len(st[b // 2]["acc"])):
+                    multiply(b, c, h)
+
+        def stt(pr, h=0):
+            acc = st[pr]["acc"][h]
+            nq = st[pr]["width"] // PACK
+            if h == 0:
+                st[pr]["v"] = keep.tile([P, PACK, P], F32, name="v", tag="e")
             nc.vector.scalar_tensor_tensor(
-                out=v[:],
-                in0=c2t[:],
+                out=st[pr]["v"][:, :, h * nq : h * nq + nq],
+                in0=c2t[:, :, h * nq : h * nq + nq],
                 scalar=asum[:, pr : pr + 1],
-                in1=st[pr]["acc"][:].rearrange("p (q c) -> p c q", c=PACK),
+                in1=acc[:].rearrange("p (q c) -> p c q", c=PACK),
                 op0=ALU.mult,
                 op1=ALU.add,
             )
-            st[pr]["v"] = v
 
         def square(pr):
             junk = epool.tile([P, PACK, P], BF16, name="junk")
@@ -242,10 +273,33 @@ def tile_modelnew_kernel(tc, x, bn_out, clusters2, out):
             nc.scalar.activation(out=junk[:], in_=st[pr]["v"][:], func=ACT.Square, accum_out=ssq[:])
             st[pr]["ssq"] = ssq
 
+        def square_half(pr, h):
+            nq = P // 2
+            junk = epool.tile([P, PACK, nq], BF16, name="junk_half", tag="junk")
+            part = tiny.tile([P, 1], F32, name="part%d" % h)
+            nc.scalar.activation(
+                out=junk[:], in_=st[pr]["v"][:, :, h * nq : h * nq + nq], func=ACT.Square, accum_out=part[:]
+            )
+            st[pr]["part%d" % h] = part
+
+        def first_part_eps(pr):
+            bias = tiny.tile([P, 1], F32, name="part_eps")
+            nc.vector.tensor_scalar(out=bias[:], in0=st[pr]["part0"][:], scalar1=EPS, scalar2=None, op0=ALU.add)
+            st[pr]["bias"] = bias
+
+        def sum_parts(pr):
+            ssq = tiny.tile([P, 1], F32, name="ssq_sum")
+            nc.vector.tensor_tensor(out=ssq[:], in0=st[pr]["part0"][:], in1=st[pr]["part1"][:], op=ALU.add)
+            st[pr]["ssq"] = ssq
+
         def rnorm(pr):
             rn = tiny.tile([P, 1], F32, name="rn")
+            halves = "bias" in st[pr]
             nc.scalar.activation(
-                out=rn[:], in_=st[pr]["ssq"][:], func=ACT.Abs_reciprocal_sqrt, bias=eps_t[:, 0:1]
+                out=rn[:],
+                in_=st[pr]["part1"][:] if halves else st[pr]["ssq"][:],
+                func=ACT.Abs_reciprocal_sqrt,
+                bias=st[pr]["bias"][:, 0:1] if halves else eps_t[:, 0:1],
             )
             st[pr]["rn"] = rn
 
@@ -265,15 +319,15 @@ def tile_modelnew_kernel(tc, x, bn_out, clusters2, out):
             )
             st[pr]["totps"] = totps
 
-        def scale(pr, bank=None):
+        def scale(pr, pool=None, tag=None):
             vs = epool.tile([P, PACK, P], F32, name="vs")
             nc.vector.tensor_scalar(
                 out=vs[:], in0=st[pr]["v"][:], scalar1=st[pr]["rn"][:, 0:1], scalar2=None, op0=ALU.mult
             )
-            if bank is None:
+            if pool is None:
                 trps = ps_tr.tile([P, PACK, P], F32, name="trps")
             else:
-                trps = ps_as.tile([P, PACK, P], F32, name="trps_late", tag=bank)
+                trps = pool.tile([P, PACK, P], F32, name="trps_late", tag=tag)
             for ch in range(PACK):
                 nc.tensor.transpose(trps[:, ch, :], vs[:, ch, :], ident[:])
             st[pr]["trps"] = trps
@@ -375,12 +429,11 @@ def tile_modelnew_kernel(tc, x, bn_out, clusters2, out):
             if (t - lag) % 2 == 0 and 0 <= (t - lag) // 2 < end:
                 step((t - lag) // 2)
 
-        for t in range(B + 1):
-            if t < B:
-                regroup_v(t)
-                regroup_s(t)
-                if t + XBUFS < B:
-                    load_x(t + XBUFS)
+        for t in range(B):
+            regroup_v(t)
+            regroup_s(t)
+            if t + XBUFS < B:
+                load_x(t + XBUFS)
             if t >= 1:
                 quant_x(t - 1)
             if 2 <= t < 10:
@@ -390,28 +443,47 @@ def tile_modelnew_kernel(tc, x, bn_out, clusters2, out):
                 acopy(0)
             if t == 10:
                 acopy(1)
-            at(t, 3, stt, 7)
-            at(t, 6, rtotal, 5)
-            at(t, 4, square, 7)
+            at(t, 3, stt, 6)
+            at(t, 6, rtotal, 4)
+            at(t, 4, square, 5)
             at(t, 6, finish, INLINE)
-            at(t, 4, rnorm, 7)
-            at(t, 5, total, 6)
-            at(t, 5, scale, 6)
+            at(t, 4, rnorm, 5)
+            at(t, 5, total, 5)
+            at(t, 5, scale, 5)
 
-        finish(4)
-        rtotal(5)
-        stt(7)
-        finish_half(5, 0)
-        square(7)
+        quantise(15, 0, 1)
+        multiply(15, 0, 0)
+        multiply(15, 0, 1)
+        stt(6)
+        square(5)
+        rnorm(5)
+        quantise(15, 1, 2, 0, HALF)
+        multiply(15, 1, 0)
+        quantise(15, 1, 2, HALF, D)
+        multiply(15, 1, 1)
+        total(5)
+        scale(5)
+        square(6)
+        rnorm(6)
+        stt(7, 0)
+        stt(7, 1)
+        square_half(7, 0)
+        square_half(7, 1)
         total(6)
-        scale(6, bank="asps0")
+        first_part_eps(7)
+        scale(6, ps_as, "asps1")
+        rtotal(4)
         rnorm(7)
+        sum_parts(7)
+        finish(4)
+        total(7)
+        scale(7, ps_acc, "acc")
+        rtotal(5)
+        finish_half(5, 0, on_vector=True)
         finish_half(5, 1)
         store(5)
-        total(7)
-        scale(7, bank="asps1")
         rtotal(6)
-        finish(6)
+        finish(6, on_vector=True)
         rtotal(7)
         finish_half(7, 0)
         finish_half(7, 1, on_vector=True)

@@ -21,7 +21,7 @@ PACK = 4
 PASSES = N // (P * PACK)
 NPAIR = B // 2
 XBUFS = 8
-NV = [224, 288] + [512] * 14
+NV = [288, 320] + [512] * 14
 INLINE = 4
 ZCHUNKS = [(0, 1), (1, 2), (2, 4), (4, 8)]
 
@@ -71,8 +71,8 @@ def tile_modelnew_kernel(tc, x, bn_out, clusters2, out):
         ident = const.tile([P, P], F32)
         mask = const.tile([P, 2], F32)
         eps_t = const.tile([P, 1], F32)
-        c2raw = const.tile([P, PACK, K], BF16)
-        c2dup = const.tile([P, PACK, 2, K], F32)
+        c2raw = const.tile([P, PACK, 2, K], BF16)
+        ident_bf = const.tile([P, P], BF16)
         c2t = const.tile([P, PACK, P], F32)
 
         zview = bn_out.rearrange("(s p j) k -> p s (j k)", p=P, j=PACK)
@@ -159,12 +159,12 @@ def tile_modelnew_kernel(tc, x, bn_out, clusters2, out):
 
         def norm(pr, parts=None):
             for c, b2 in parts or [(0, 0), (0, 1), (1, 0), (1, 1)]:
-                    nc.vector.tensor_tensor(
-                        out=pg[:, 4 * pr + 2 * c + b2, :, :].rearrange("p (w i) j -> p w j i", i=2),
-                        in0=es[pr][:, :, c, b2, :].rearrange("p j (w i) -> p w j i", i=2),
-                        in1=rinvs[pr][:, c, b2, :].unsqueeze(1).unsqueeze(3).to_broadcast([P, K // 2, PACK, 2]),
-                        op=ALU.mult,
-                    )
+                nc.vector.tensor_tensor(
+                    out=pg[:, 4 * pr + 2 * c + b2, :, :].rearrange("p (w i) j -> p w j i", i=2),
+                    in0=es[pr][:, :, c, b2, :].rearrange("p j (w i) -> p w j i", i=2),
+                    in1=rinvs[pr][:, c, b2, :].unsqueeze(1).unsqueeze(3).to_broadcast([P, K // 2, PACK, 2]),
+                    op=ALU.mult,
+                )
 
         def quant_p(g0, g1):
             w0 = 384 * (g0 // 4) + 192 * ((g0 % 4) // 2) + 128 * (g0 % 2)
@@ -359,11 +359,9 @@ def tile_modelnew_kernel(tc, x, bn_out, clusters2, out):
             finish_half(pr, 1, on_vector)
             store(pr)
 
-        nc.sync.dma_start(
-            out=c2raw[:].rearrange("p c k -> p (c k)"),
-            in_=clusters2[0].rearrange("(q c) k -> q (c k)", c=PACK),
-        )
         load_z(0, 0, 1)
+        for b2 in range(2):
+            nc.scalar.dma_start(out=c2raw[:, :, b2, :], in_=clusters2[0].rearrange("(q c) k -> q c k", c=PACK))
         load_z(0, 1, 2 * PASSES)
         for ch in range(1, len(ZCHUNKS)):
             load_z(ch)
@@ -372,16 +370,16 @@ def tile_modelnew_kernel(tc, x, bn_out, clusters2, out):
 
         nc.vector.memset(pw[:, :, :, 64:128].bitcast(I32), 0)
         nc.vector.memset(pscale[:, :, :, 64:128].bitcast(I32), 0)
+        make_identity(nc, ident_bf[:])
         make_identity(nc, ident[:])
         nc.gpsimd.memset(mask[:], 0.0)
         nc.gpsimd.memset(mask[0:64, 0:1], 1.0)
         nc.gpsimd.memset(mask[64:128, 1:2], 1.0)
         nc.gpsimd.memset(eps_t[:], EPS)
 
-        nc.scalar.copy(out=c2dup[:], in_=c2raw[:].unsqueeze(2).to_broadcast([P, PACK, 2, K]))
-        c2ps = ps_tr.tile([P, PACK, P], F32, name="trps")
+        c2ps = ps_tr.tile([P, PACK, P], BF16, name="c2ps", tag="trps")
         for ch in range(PACK):
-            nc.tensor.transpose(c2ps[:, ch, :], c2dup[:, ch, :, :].rearrange("p b k -> p (b k)"), ident[:])
+            nc.tensor.transpose(c2ps[:, ch, :], c2raw[:, ch, :, :].rearrange("p b k -> p (b k)"), ident_bf[:])
         m1 = max_steps(1)
         m2 = max_steps(2)
         m3 = max_steps(3)
@@ -392,10 +390,10 @@ def tile_modelnew_kernel(tc, x, bn_out, clusters2, out):
         first_max(3)
         exps(0)
         m1[1]()
-        nc.vector.tensor_copy(out=c2t[:], in_=c2ps[:])
         m1[2]()
         m1[3]()
         exps(1)
+        nc.scalar.copy(out=c2t[:], in_=c2ps[:])
         m2[0]()
         recip(0)
         a_sum(0)

@@ -360,22 +360,25 @@ def tile_modelnew_kernel(tc, x, bn_out, clusters2, out):
             store(pr)
 
         load_z(0, 0, 1)
-        for b2 in range(2):
-            nc.scalar.dma_start(out=c2raw[:, :, b2, :], in_=clusters2[0].rearrange("(q c) k -> q c k", c=PACK))
         load_z(0, 1, 2 * PASSES)
-        for ch in range(1, len(ZCHUNKS)):
-            load_z(ch)
+        load_z(1)
+        for b2 in range(2):
+            nc.sync.dma_start(out=c2raw[:, :, b2, :], in_=clusters2[0].rearrange("(q c) k -> q c k", c=PACK))
+        load_z(2)
+        load_z(3)
         for b in range(XBUFS):
             load_x(b)
 
         nc.vector.memset(pw[:, :, :, 64:128].bitcast(I32), 0)
         nc.vector.memset(pscale[:, :, :, 64:128].bitcast(I32), 0)
+        nc.gpsimd.memset(eps_t[:], EPS)
         make_identity(nc, ident_bf[:])
         make_identity(nc, ident[:])
         nc.gpsimd.memset(mask[:], 0.0)
         nc.gpsimd.memset(mask[0:64, 0:1], 1.0)
         nc.gpsimd.memset(mask[64:128, 1:2], 1.0)
-        nc.gpsimd.memset(eps_t[:], EPS)
+        ready = tiny.tile([P, 1], F32, name="ready")
+        nc.scalar.activation(out=ready[:], in_=eps_t[:], func=ACT.Exp)
 
         c2ps = ps_tr.tile([P, PACK, P], BF16, name="c2ps", tag="trps")
         for ch in range(PACK):

@@ -21,7 +21,7 @@ PACK = 4
 PASSES = N // (P * PACK)
 NPAIR = B // 2
 XBUFS = 8
-NV = [288, 320] + [512] * 14
+NV = [416, 448] + [512] * 14
 INLINE = 4
 ZCHUNKS = [(0, 1), (1, 2), (2, 4), (4, 8)]
 
@@ -333,6 +333,30 @@ def tile_modelnew_kernel(tc, x, bn_out, clusters2, out):
             st[pr]["trps"] = trps
             st[pr]["o"] = opool.tile([P, 2, PACK, K], F32, name="o")
 
+        def scale_apart(pr, places):
+            vs = epool.tile([P, PACK, P], F32, name="vs")
+            nc.vector.tensor_scalar(
+                out=vs[:], in0=st[pr]["v"][:], scalar1=st[pr]["rn"][:, 0:1], scalar2=None, op0=ALU.mult
+            )
+            st[pr]["trps"] = []
+            for h in range(2):
+                pool, tag = places[h]
+                trps = pool.tile([P, PACK // 2, P], F32, name="trps_half%d" % h, tag=tag)
+                for ch in range(PACK // 2):
+                    nc.tensor.transpose(trps[:, ch, :], vs[:, PACK // 2 * h + ch, :], ident[:])
+                st[pr]["trps"].append(trps)
+            st[pr]["o"] = opool.tile([P, 2, PACK, K], F32, name="o")
+
+        def finish_apart(pr, h, on_vector=False):
+            for b2 in range(2):
+                dst = st[pr]["o"][:, b2, PACK // 2 * h : PACK // 2 * (h + 1), :]
+                src = st[pr]["trps"][h][:, :, K * b2 : K * b2 + K]
+                r2 = st[pr]["r2"][:, b2 : b2 + 1]
+                if on_vector:
+                    nc.vector.tensor_scalar(out=dst, in0=src, scalar1=r2, scalar2=None, op0=ALU.mult)
+                else:
+                    nc.scalar.activation(out=dst, in_=src, func=ACT.Copy, scale=r2)
+
         def rtotal(pr):
             r2 = tiny.tile([P, 2], F32, name="r2")
             nc.scalar.activation(
@@ -476,16 +500,16 @@ def tile_modelnew_kernel(tc, x, bn_out, clusters2, out):
         rtotal(4)
         rnorm(7)
         sum_parts(7)
-        finish(4)
+        finish_half(4, 0)
         total(7)
-        scale(7, ps_acc, "acc")
+        scale_apart(7, [(ps_acc, "acc"), (ps_as, "asps0")])
         rtotal(5)
-        finish_half(5, 0, on_vector=True)
-        finish_half(5, 1)
-        store(5)
         rtotal(6)
-        finish(6, on_vector=True)
+        finish_half(4, 1)
+        store(4)
+        finish(5, on_vector=True)
+        finish(6)
         rtotal(7)
-        finish_half(7, 0)
-        finish_half(7, 1, on_vector=True)
+        finish_apart(7, 0)
+        finish_apart(7, 1, on_vector=True)
         store(7)

from contextlib import ExitStack

import concourse.mybir as mybir
from concourse.masks import make_identity

F32 = mybir.dt.float32
BF16 = mybir.dt.bfloat16
U32 = mybir.dt.uint32
U8 = mybir.dt.uint8
I32 = mybir.dt.int32
FP8X4 = mybir.dt.float8_e4m3fn_x4
ALU = mybir.AluOpType
ACT = mybir.ActivationFunctionType
AX = mybir.AxisListType

B, N, D, K = 16, 1024, 512, 64
EPS = 1e-12
HALF = D // 2
P = 128
PACK = 4
PASSES = N // (P * PACK)
NPAIR = B // 2
XBUFS = 8
NV = [416, 448] + [512] * 14
INLINE = 4
ZCHUNKS = [(0, 1), (1, 2), (2, 4), (4, 8)]

FLOPS = 2 * B * N * K * D


def tile_modelnew_kernel(tc, x, bn_out, clusters2, out):
    nc = tc.nc
    with ExitStack() as ctx:
        const = ctx.enter_context(tc.tile_pool(name="const", bufs=1))
        xpool = ctx.enter_context(tc.tile_pool(name="xraw", bufs=XBUFS))
        gpool = ctx.enter_context(tc.tile_pool(name="grouped", bufs=4))
        wpool = ctx.enter_context(tc.tile_pool(name="xwords", bufs=4))
        mpool = ctx.enter_context(tc.tile_pool(name="maxes", bufs=1))
        epool = ctx.enter_context(tc.tile_pool(name="epi", bufs=3))
        tiny = ctx.enter_context(tc.tile_pool(name="tiny", bufs=4))
        opool = ctx.enter_context(tc.tile_pool(name="outs", bufs=5))
        keep = ctx.enter_context(tc.tile_pool(name="keep", bufs=NPAIR))
        ps_acc = ctx.enter_context(tc.psum_pool(name="ps_acc", bufs=2))
        ps_tr = ctx.enter_context(tc.psum_pool(name="ps_tr", bufs=2))
        ps_as = ctx.enter_context(tc.psum_pool(name="ps_as", bufs=1))
        ps_tot = ctx.enter_context(tc.psum_pool(name="ps_tot", bufs=2))
        ctx.enter_context(tc.manual_schedule())

        zts = []
        negmaxes = []
        for ch in range(len(ZCHUNKS)):
            ns = (ZCHUNKS[ch][1] - ZCHUNKS[ch][0]) * 2 * PASSES
            zts.append(const.tile([P, ns, PACK, K], BF16, name="zt%d" % ch))
            negmaxes.append(const.tile([P, ns * PACK], F32, name="negmax%d" % ch))
        chunk_of = {}
        for ch in range(len(ZCHUNKS)):
            for pr in range(ZCHUNKS[ch][0], ZCHUNKS[ch][1]):
                chunk_of[pr] = ch
        es = []
        sumss = []
        rinvs = []
        for pr in range(NPAIR):
            es.append(keep.tile([P, PACK, PASSES, 2, K], F32, name="e"))
            sumss.append(keep.tile([P, PASSES, 2, PACK], F32, name="sums"))
            rinvs.append(keep.tile([P, PASSES, 2, PACK], F32, name="rinv"))
        pg = const.tile([P, NPAIR * PASSES * 2, K, PACK], BF16, align_bytes=64)
        pw = const.tile([P, NPAIR, PASSES, 192], U32, align_bytes=64)
        pscale = const.tile([P, NPAIR, PASSES, 192], U8, align_bytes=64)
        asum = const.tile([P, NPAIR], F32)
        asps = [ps_as.tile([P, 4, 2], F32, name="asps0"), ps_as.tile([P, 4, 2], F32, name="asps1")]
        ident = const.tile([P, P], F32)
        mask = const.tile([P, 2], F32)
        eps_t = const.tile([P, 1], F32)
        c2raw = const.tile([P, PACK, 2, K], BF16)
        ident_bf = const.tile([P, P], BF16)
        c2t = const.tile([P, PACK, P], F32)

        zview = bn_out.rearrange("(s p j) k -> p s (j k)", p=P, j=PACK)

        def load_z(ch, first=0, end=None):
            s0 = ZCHUNKS[ch][0] * 2 * PASSES
            s1 = ZCHUNKS[ch][1] * 2 * PASSES
            if end is None:
                end = s1 - s0
            nc.sync.dma_start(
                out=zts[ch][:, first:end, :, :].rearrange("p s j k -> p s (j k)"), in_=zview[:, s0 + first : s0 + end, :]
            )

        xraw = {}

        def load_x(b):
            raw = xpool.tile([P, PASSES, PACK, D], BF16, name="raw")
            xv = x[b].rearrange("(c p j) d -> c p (j d)", c=PASSES, p=P, j=PACK)
            for c in range(PASSES):
                nc.sync.dma_start(out=raw[:, c, :, :].rearrange("p j d -> p (j d)"), in_=xv[c])
            xraw[b] = raw

        def max_steps(ch):
            ns = (ZCHUNKS[ch][1] - ZCHUNKS[ch][0]) * 2 * PASSES * PACK
            zc = zts[ch][:].rearrange("p s j k -> p (s j) k")
            t1 = mpool.tile([P, ns, 32], BF16, name="t1_%d" % ch)
            t2 = mpool.tile([P, ns, 16], BF16, name="t2_%d" % ch)
            t3 = mpool.tile([P, ns, 8], BF16, name="t3_%d" % ch)
            return [
                lambda: nc.vector.tensor_tensor(out=t1[:], in0=zc[:, :, 0:32], in1=zc[:, :, 32:64], op=ALU.max),
                lambda: nc.vector.tensor_tensor(out=t2[:], in0=t1[:, :, 0:16], in1=t1[:, :, 16:32], op=ALU.max),
                lambda: nc.vector.tensor_tensor(out=t3[:], in0=t2[:, :, 0:8], in1=t2[:, :, 8:16], op=ALU.max),
                lambda: nc.vector.tensor_reduce(
                    out=negmaxes[ch][:], in_=t3[:], axis=AX.X, op=ALU.max, negate=True
                ),
            ]

        def first_max(s):
            nc.vector.tensor_reduce(
                out=negmaxes[0][:, PACK * s : PACK * s + PACK], in_=zts[0][:, s, :, :], axis=AX.X, op=ALU.max, negate=True
            )

        def exps(pr):
            ch = chunk_of[pr]
            for b2 in range(2):
                for c in range(PASSES):
                    s = (2 * (pr - ZCHUNKS[ch][0]) + b2) * PASSES + c
                    for j in range(PACK):
                        i = s * PACK + j
                        nc.scalar.activation(
                            out=es[pr][:, j, c, b2, :],
                            in_=zts[ch][:, s, j, :],
                            func=ACT.Exp,
                            bias=negmaxes[ch][:, i : i + 1],
                            scale=1.0,
                            accum_out=sumss[pr][:, c, b2, j : j + 1],
                        )

        def recip(pr):
            nc.vector.reciprocal(out=rinvs[pr][:], in_=sumss[pr][:])

        def a_sum_step(pr, i):
            nc.tensor.matmul(
                out=asps[pr // 4][:, pr % 4, :],
                lhsT=es[pr][:, i // PASSES, i % PASSES, :, :].rearrange("p b k -> p (b k)"),
                rhs=rinvs[pr][:, i % PASSES, :, i // PASSES],
                start=(i == 0),
                stop=(i == PASSES * PACK - 1),
            )

        def a_sum(pr):
            for i in range(PASSES * PACK):
                a_sum_step(pr, i)

        def acopy(half):
            for b2 in range(2):
                nc.vector.tensor_scalar(
                    out=asum[64 * b2 : 64 * b2 + 64, 4 * half : 4 * half + 4],
                    in0=asps[half][64 * b2 : 64 * b2 + 64, :, b2],
                    scalar1=-1.0,
                    scalar2=None,
                    op0=ALU.mult,
                )

        def norm(pr, parts=None):
            for c, b2 in parts or [(0, 0), (0, 1), (1, 0), (1, 1)]:
                nc.vector.tensor_tensor(
                    out=pg[:, 4 * pr + 2 * c + b2, :, :].rearrange("p (w i) j -> p w j i", i=2),
                    in0=es[pr][:, :, c, b2, :].rearrange("p j (w i) -> p w j i", i=2),
                    in1=rinvs[pr][:, c, b2, :].unsqueeze(1).unsqueeze(3).to_broadcast([P, K // 2, PACK, 2]),
                    op=ALU.mult,
                )

        def quant_p(g0, g1):
            w0 = 384 * (g0 // 4) + 192 * ((g0 % 4) // 2) + 128 * (g0 % 2)
            w1 = w0 + K * (g1 - g0)
            nc.vector.quantize_mx(
                out=pw[:].rearrange("p r c w -> p (r c w)")[:, w0:w1].bitcast(FP8X4),
                scales=pscale[:].rearrange("p r c w -> p (r c w)")[:, w0:w1],
                in_=pg[:, g0:g1, :, :].rearrange("p g k j -> p (g k j)"),
            )

        def quant_p_pair(pr):
            if pr < 0:
                return
            quant_p(max(4 * pr - 1, 0), 4 * pr + 1)
            quant_p(4 * pr + 1, 4 * pr + 3)

        groupeds = {}

        def regroup(copy, b, c, d0, d1):
            if d0 < d1:
                copy(
                    out=groupeds[b][:, c, d0:d1, :].rearrange("p (w i) t -> p w t i", i=4),
                    in_=xraw[b][:, c, :, d0:d1].rearrange("p t (w i) -> p w t i", i=4),
                )

        def regroup_v(b):
            groupeds[b] = gpool.tile([P, PASSES, D, PACK], BF16, name="grouped", align_bytes=64)
            regroup(nc.vector.tensor_copy, b, 0, 0, min(NV[b], D))
            regroup(nc.vector.tensor_copy, b, 1, 0, NV[b] - D)

        def regroup_s(b):
            regroup(nc.scalar.copy, b, 0, NV[b], D)
            regroup(nc.scalar.copy, b, 1, max(NV[b] - D, 0), D)

        st = {}

        def start_acc(pr):
            if pr < NPAIR - 1:
                st[pr] = {"width": D, "acc": [ps_acc.tile([P, D], F32, name="acc")]}
            else:
                st[pr] = {
                    "width": HALF,
                    "acc": [
                        ps_acc.tile([P, HALF], F32, name="acc_first", tag="acc"),
                        ps_as.tile([P, HALF], F32, name="acc_second", tag="asps0"),
                    ]
                }

        words = {}

        def quantise(b, c0, c1, d0=0, d1=D):
            if b not in words:
                xw = wpool.tile([P, PASSES, D], U32, name="xw", align_bytes=64)
                xs = wpool.tile([P, PASSES, D], U8, name="xs", align_bytes=64)
                words[b] = (xw, xs)
            xw, xs = words[b]
            nc.vector.quantize_mx(
                out=xw[:].rearrange("p c d -> p (c d)")[:, c0 * D + d0 : (c1 - 1) * D + d1].bitcast(FP8X4),
                scales=xs[:].rearrange("p c d -> p (c d)")[:, c0 * D + d0 : (c1 - 1) * D + d1],
                in_=groupeds[b][:].rearrange("p c d t -> p (c d t)")[
                    :, PACK * (c0 * D + d0) : PACK * ((c1 - 1) * D + d1)
                ],
            )

        def multiply(b, c, h=0):
            pr = b // 2
            b2 = b % 2
            xw, xs = words[b]
            acc = st[pr]["acc"][h]
            cols = slice(h * HALF, h * HALF + st[pr]["width"])
            nc.tensor.matmul_mx(
                out=acc[:],
                lhsT=pw[:, pr, c, 64 * b2 : 64 * b2 + P].bitcast(FP8X4),
                lhsT_scale=pscale[:, pr, c, 64 * b2 : 64 * b2 + P],
                rhs=xw[:, c, cols].bitcast(FP8X4),
                rhs_scale=xs[:, c, cols],
                start=(b2 == 0 and c == 0),
                stop=(b2 == 1 and c == PASSES - 1),
            )

        def quant_x(b):
            if b % 2 == 0:
                start_acc(b // 2)
            quantise(b, 0, PASSES)
            for c in range(PASSES):
                for h in range(len(st[b // 2]["acc"])):
                    multiply(b, c, h)

        def stt(pr, h=0):
            acc = st[pr]["acc"][h]
            nq = st[pr]["width"] // PACK
            if h == 0:
                st[pr]["v"] = keep.tile([P, PACK, P], F32, name="v", tag="e")
            nc.vector.scalar_tensor_tensor(
                out=st[pr]["v"][:, :, h * nq : h * nq + nq],
                in0=c2t[:, :, h * nq : h * nq + nq],
                scalar=asum[:, pr : pr + 1],
                in1=acc[:].rearrange("p (q c) -> p c q", c=PACK),
                op0=ALU.mult,
                op1=ALU.add,
            )

        def square(pr):
            junk = epool.tile([P, PACK, P], BF16, name="junk")
            ssq = tiny.tile([P, 1], F32, name="ssq")
            nc.scalar.activation(out=junk[:], in_=st[pr]["v"][:], func=ACT.Square, accum_out=ssq[:])
            st[pr]["ssq"] = ssq

        def square_half(pr, h):
            nq = P // 2
            junk = epool.tile([P, PACK, nq], BF16, name="junk_half", tag="junk")
            part = tiny.tile([P, 1], F32, name="part%d" % h)
            nc.scalar.activation(
                out=junk[:], in_=st[pr]["v"][:, :, h * nq : h * nq + nq], func=ACT.Square, accum_out=part[:]
            )
            st[pr]["part%d" % h] = part

        def first_part_eps(pr):
            bias = tiny.tile([P, 1], F32, name="part_eps")
            nc.vector.tensor_scalar(out=bias[:], in0=st[pr]["part0"][:], scalar1=EPS, scalar2=None, op0=ALU.add)
            st[pr]["bias"] = bias

        def sum_parts(pr):
            ssq = tiny.tile([P, 1], F32, name="ssq_sum")
            nc.vector.tensor_tensor(out=ssq[:], in0=st[pr]["part0"][:], in1=st[pr]["part1"][:], op=ALU.add)
            st[pr]["ssq"] = ssq

        def rnorm(pr):
            rn = tiny.tile([P, 1], F32, name="rn")
            halves = "bias" in st[pr]
            nc.scalar.activation(
                out=rn[:],
                in_=st[pr]["part1"][:] if halves else st[pr]["ssq"][:],
                func=ACT.Abs_reciprocal_sqrt,
                bias=st[pr]["bias"][:, 0:1] if halves else eps_t[:, 0:1],
            )
            st[pr]["rn"] = rn

        def total(pr):
            u = tiny.tile([P, 2], F32, name="u")
            nc.vector.tensor_scalar(
                out=u[:],
                in0=mask[:],
                scalar1=st[pr]["ssq"][:, 0:1],
                scalar2=st[pr]["rn"][:, 0:1],
                op0=ALU.mult,
                op1=ALU.mult,
            )
            totps = ps_tot.tile([P, 2], F32, name="totps")
            nc.tensor.matmul(
                out=totps[:], lhsT=st[pr]["rn"][:, 0:1].to_broadcast([P, P]), rhs=u[:], start=True, stop=True
            )
            st[pr]["totps"] = totps

        def scale(pr, pool=None, tag=None):
            vs = epool.tile([P, PACK, P], F32, name="vs")
            nc.vector.tensor_scalar(
                out=vs[:], in0=st[pr]["v"][:], scalar1=st[pr]["rn"][:, 0:1], scalar2=None, op0=ALU.mult
            )
            if pool is None:
                trps = ps_tr.tile([P, PACK, P], F32, name="trps")
            else:
                trps = pool.tile([P, PACK, P], F32, name="trps_late", tag=tag)
            for ch in range(PACK):
                nc.tensor.transpose(trps[:, ch, :], vs[:, ch, :], ident[:])
            st[pr]["trps"] = trps
            st[pr]["o"] = opool.tile([P, 2, PACK, K], F32, name="o")

        def scale_apart(pr, places):
            vs = epool.tile([P, PACK, P], F32, name="vs")
            nc.vector.tensor_scalar(
                out=vs[:], in0=st[pr]["v"][:], scalar1=st[pr]["rn"][:, 0:1], scalar2=None, op0=ALU.mult
            )
            st[pr]["trps"] = []
            for h in range(2):
                pool, tag = places[h]
                trps = pool.tile([P, PACK // 2, P], F32, name="trps_half%d" % h, tag=tag)
                for ch in range(PACK // 2):
                    nc.tensor.transpose(trps[:, ch, :], vs[:, PACK // 2 * h + ch, :], ident[:])
                st[pr]["trps"].append(trps)
            st[pr]["o"] = opool.tile([P, 2, PACK, K], F32, name="o")

        def finish_apart(pr, h, on_vector=False):
            for b2 in range(2):
                dst = st[pr]["o"][:, b2, PACK // 2 * h : PACK // 2 * (h + 1), :]
                src = st[pr]["trps"][h][:, :, K * b2 : K * b2 + K]
                r2 = st[pr]["r2"][:, b2 : b2 + 1]
                if on_vector:
                    nc.vector.tensor_scalar(out=dst, in0=src, scalar1=r2, scalar2=None, op0=ALU.mult)
                else:
                    nc.scalar.activation(out=dst, in_=src, func=ACT.Copy, scale=r2)

        def rtotal(pr):
            r2 = tiny.tile([P, 2], F32, name="r2")
            nc.scalar.activation(
                out=r2[:], in_=st[pr]["totps"][:], func=ACT.Abs_reciprocal_sqrt, bias=eps_t[:, 0:1]
            )
            st[pr]["r2"] = r2

        def finish_half(pr, b2, on_vector=False):
            src = st[pr]["trps"][:, :, K * b2 : K * b2 + K]
            r2 = st[pr]["r2"][:, b2 : b2 + 1]
            if on_vector:
                nc.vector.tensor_scalar(out=st[pr]["o"][:, b2], in0=src, scalar1=r2, scalar2=None, op0=ALU.mult)
            else:
                nc.scalar.activation(out=st[pr]["o"][:, b2], in_=src, func=ACT.Copy, scale=r2)

        def store(pr):
            nc.sync.dma_start(
                out=out[2 * pr : 2 * pr + 2, :].rearrange("b (q r) -> q b r", q=P),
                in_=st[pr]["o"][:].rearrange("p b c k -> p b (c k)"),
            )

        def finish(pr, on_vector=False):
            finish_half(pr, 0, on_vector)
            finish_half(pr, 1, on_vector)
            store(pr)

        load_z(0, 0, 1)
        load_z(0, 1, 2 * PASSES)
        load_z(1)
        for b2 in range(2):
            nc.sync.dma_start(out=c2raw[:, :, b2, :], in_=clusters2[0].rearrange("(q c) k -> q c k", c=PACK))
        load_z(2)
        load_z(3)
        for b in range(XBUFS):
            load_x(b)

        nc.vector.memset(pw[:, :, :, 64:128].bitcast(I32), 0)
        nc.vector.memset(pscale[:, :, :, 64:128].bitcast(I32), 0)
        nc.gpsimd.memset(eps_t[:], EPS)
        make_identity(nc, ident_bf[:])
        make_identity(nc, ident[:])
        nc.gpsimd.memset(mask[:], 0.0)
        nc.gpsimd.memset(mask[0:64, 0:1], 1.0)
        nc.gpsimd.memset(mask[64:128, 1:2], 1.0)
        ready = tiny.tile([P, 1], F32, name="ready")
        nc.scalar.activation(out=ready[:], in_=eps_t[:], func=ACT.Exp)

        c2ps = ps_tr.tile([P, PACK, P], BF16, name="c2ps", tag="trps")
        for ch in range(PACK):
            nc.tensor.transpose(c2ps[:, ch, :], c2raw[:, ch, :, :].rearrange("p b k -> p (b k)"), ident_bf[:])
        m1 = max_steps(1)
        m2 = max_steps(2)
        m3 = max_steps(3)
        first_max(0)
        first_max(1)
        first_max(2)
        m1[0]()
        first_max(3)
        exps(0)
        m1[1]()
        m1[2]()
        m1[3]()
        exps(1)
        nc.scalar.copy(out=c2t[:], in_=c2ps[:])
        m2[0]()
        recip(0)
        a_sum(0)
        m2[1]()
        norm(0, [(0, 0)])
        m2[2]()
        norm(0, [(0, 1)])
        m2[3]()
        exps(2)
        norm(0, [(1, 0)])
        m3[0]()
        norm(0, [(1, 1)])
        m3[1]()
        for pr in range(1, NPAIR):
            recip(pr)
            if pr < 4:
                a_sum(pr)
            quant_p_pair(pr - 1)
            if pr == 1:
                m3[2]()
            norm(pr, [(0, 0), (0, 1)])
            if pr == 1:
                m3[3]()
            norm(pr, [(1, 0), (1, 1)])
            if pr + 2 < NPAIR:
                exps(pr + 2)
        quant_p_pair(NPAIR - 1)
        quant_p(4 * NPAIR - 1, 4 * NPAIR)

        def at(t, lag, step, end):
            if (t - lag) % 2 == 0 and 0 <= (t - lag) // 2 < end:
                step((t - lag) // 2)

        for t in range(B):
            regroup_v(t)
            regroup_s(t)
            if t + XBUFS < B:
                load_x(t + XBUFS)
            if t >= 1:
                quant_x(t - 1)
            if 2 <= t < 10:
                for i in range(4 * (t - 2), 4 * (t - 2) + 4):
                    a_sum_step(4 + i // 8, i % 8)
            if t == 2:
                acopy(0)
            if t == 10:
                acopy(1)
            at(t, 3, stt, 6)
            at(t, 6, rtotal, 4)
            at(t, 4, square, 5)
            at(t, 6, finish, INLINE)
            at(t, 4, rnorm, 5)
            at(t, 5, total, 5)
            at(t, 5, scale, 5)

        quantise(15, 0, 1)
        multiply(15, 0, 0)
        multiply(15, 0, 1)
        stt(6)
        square(5)
        rnorm(5)
        quantise(15, 1, 2, 0, HALF)
        multiply(15, 1, 0)
        quantise(15, 1, 2, HALF, D)
        multiply(15, 1, 1)
        total(5)
        scale(5)
        square(6)
        rnorm(6)
        stt(7, 0)
        stt(7, 1)
        square_half(7, 0)
        square_half(7, 1)
        total(6)
        first_part_eps(7)
        scale(6, ps_as, "asps1")
        rtotal(4)
        rnorm(7)
        sum_parts(7)
        finish_half(4, 0)
        total(7)
        scale_apart(7, [(ps_acc, "acc"), (ps_as, "asps0")])
        rtotal(5)
        rtotal(6)
        finish_half(4, 1)
        store(4)
        finish(5, on_vector=True)
        finish(6)
        rtotal(7)
        finish_apart(7, 0)
        finish_apart(7, 1, on_vector=True)
        store(7)
